import numpy as np
import ml_dtypes


def mxq(x, axis, fmt="e4m3"):
    dtype, down = {"e4m3": (ml_dtypes.float8_e4m3fn, 7), "e5m2": (ml_dtypes.float8_e5m2, 14)}[fmt]
    v = np.moveaxis(np.asarray(x, np.float32).astype(ml_dtypes.bfloat16).astype(np.float64), axis, -1)
    blocks = v.reshape(v.shape[:-1] + (-1, 32))
    amax = np.abs(blocks).max(-1, keepdims=True)
    byte = np.maximum(np.where(amax > 0, np.frexp(amax)[1] - 1 + 127, 0) - down, 1)
    scale = np.exp2(byte - 127.0)
    codes = (blocks / scale).astype(np.float32).astype(dtype).astype(np.float64)
    return np.moveaxis((codes * scale).reshape(v.shape), -1, axis)


WIDE = False


def mx_kscale(k):
    if not WIDE:
        return np.ones(k)
    levels = np.array([10, -10, 5, -5, 0])
    a = np.random.permutation(np.resize(levels, k // 512 * 4)).reshape(k // 512, 4)
    idx = np.arange(k)
    return np.exp2(a[idx // 512, idx % 128 // 32])


BF16 = ml_dtypes.bfloat16


def bf(x):
    return np.asarray(x, np.float32).astype(BF16)


def f64(x):
    return np.asarray(x).astype(np.float64)


E2M1 = np.array([0.0, 0.5, 1.0, 1.5, 2.0, 3.0, 4.0, 6.0, -0.0, -0.5, -1.0, -1.5, -2.0, -3.0, -4.0, -6.0])


def pack_weight(w, fmt):
    k, n = w.shape
    w = f64(bf(w)).reshape(k // 32, 32, n)
    amax = np.abs(w).max(1)
    if fmt == "e4m3":
        byte = np.frexp(amax)[1] - 1 + 127 - 7
    else:
        mant, ex = np.frexp(amax / 6.0)
        byte = np.where(mant > 0.5, ex, ex - 1) + 127
    byte = np.clip(np.where(amax > 0, byte, 1), 1, 254)
    scaled = (w * np.exp2(127.0 - byte)[:, None, :]).reshape(k, n).astype(np.float32)
    by_word = np.ascontiguousarray(scaled.reshape(k // 512, 128, 4, n).transpose(0, 1, 3, 2))
    if fmt == "e4m3":
        words = by_word.astype(ml_dtypes.float8_e4m3fn).view(np.uint8)
    else:
        c = by_word.astype(ml_dtypes.float4_e2m1fn).view(np.uint8) & 0xF
        words = c[..., 0::2] | (c[..., 1::2] << 4)
    return np.ascontiguousarray(words), np.ascontiguousarray(byte.astype(np.uint8).reshape(k // 512, 16, n))


def unpack_weight(words, scales, fmt):
    g, p, n, _ = words.shape
    if fmt == "e4m3":
        vals = np.ascontiguousarray(words).view(ml_dtypes.float8_e4m3fn).astype(np.float64)
    else:
        nib = np.empty((g, p, n, 4), np.uint8)
        nib[..., 0::2] = words & 0xF
        nib[..., 1::2] = words >> 4
        vals = E2M1[nib]
    vals = vals * np.repeat(np.exp2(scales.astype(np.float64) - 127.0), 8, axis=1)[..., None]
    return vals.transpose(0, 1, 3, 2).reshape(g * 512, n)

def pack4(w):
    words, scales = pack_weight(w, "e2m1")
    return words.reshape(words.shape[0], 128, -1), scales


def unpack4(words, scales):
    return unpack_weight(words.reshape(words.shape[0], 128, -1, 2), scales, "e2m1")


N, P, D, E, F = 256, 3, 512, 16384, 512
BN_EPS = 1e-5


def setup_inputs():
    t = mx_kscale(E)
    h = 1.2 * np.random.standard_normal((N, P, E)) + 0.6 * np.random.standard_normal((1, P, E))
    w1b_words, w1b_scales = pack4(np.random.standard_normal((E, F)) / np.sqrt(E) / t[:, None])
    w2b_words, w2b_scales = pack4(np.random.standard_normal((E, F)) / np.sqrt(E) / t[:, None])
    return {"h_sage": bf(h * t),
            "w1b_words": w1b_words,
            "w1b_scales": w1b_scales,
            "w2b_words": w2b_words,
            "w2b_scales": w2b_scales,
            "gamma": bf(1.0 + 0.2 * np.random.standard_normal(F)),
            "beta": bf(0.3 * np.random.standard_normal(F))}


def reference(h_sage, w1b_words, w1b_scales, w2b_words, w2b_scales, gamma, beta):
    h = f64(h_sage)
    neigh = (h.sum(axis=1, keepdims=True) - h) * 0.5
    out = (mxq(h[:, 0, :], 1, "e4m3") @ unpack4(w2b_words, w2b_scales)) + (mxq(neigh[:, 0, :], 1, "e4m3") @ unpack4(w1b_words, w1b_scales))
    mean = out.mean(axis=0)
    var = out.var(axis=0)
    out = (out - mean) / np.sqrt(var + BN_EPS) * f64(gamma) + f64(beta)
    return 1.0 / (1.0 + np.exp(-out))

@@ -1,0 +1,296 @@
+from contextlib import ExitStack
+
+import concourse.mybir as mybir
+from concourse.masks import make_identity
+
+F32 = mybir.dt.float32
+BF16 = mybir.dt.bfloat16
+I32 = mybir.dt.int32
+U32 = mybir.dt.uint32
+U8 = mybir.dt.uint8
+FP8X4 = mybir.dt.float8_e4m3fn_x4
+FP4X4 = mybir.dt.float4_e2m1fn_x4
+ACT = mybir.ActivationFunctionType
+ALU = mybir.AluOpType
+
+P = 128
+PACK = 4
+GROUP_K = P * PACK
+ITEMS = 256
+ITEM_TILES = ITEMS // P
+HOPS = 3
+FEATURES = 16384
+COLS = 512
+COL_TILES = COLS // P
+BN_EPS = 1e-5
+
+GROUPS = FEATURES // GROUP_K
+STEP_GROUPS = 2
+STEPS = GROUPS // STEP_GROUPS
+CHUNK_GROUPS = 4
+CHUNK_STEPS = CHUNK_GROUPS // STEP_GROUPS
+CHUNKS = GROUPS // CHUNK_GROUPS
+CHUNK_K = CHUNK_GROUPS * GROUP_K
+QUARTER_GROUPS = 8
+QUARTER_CHUNKS = QUARTER_GROUPS // CHUNK_GROUPS
+QUARTERS = GROUPS // QUARTER_GROUPS
+GROUP_WORDS = GROUP_K // 2
+
+SELF = 0
+NEIGH = 1
+OPERANDS = (SELF, NEIGH)
+
+H_AHEAD = 3
+W_AHEAD = 2
+
+FLOPS = 2 * 2 * ITEMS * FEATURES * COLS
+
+
+def tile_dogtaitujuanji_pb_k_kernel(
+    tc, h_sage, w1b_words, w1b_scales, w2b_words, w2b_scales, gamma, beta, out
+):
+    nc = tc.nc
+    words_dram = (w2b_words, w1b_words)
+    scales_dram = (w2b_scales, w1b_scales)
+
+    with ExitStack() as stack:
+        const = stack.enter_context(tc.tile_pool(name="const", bufs=1))
+        h_pool = stack.enter_context(tc.tile_pool(name="h", bufs=(H_AHEAD + 1) * ITEM_TILES))
+        w_pool = stack.enter_context(tc.tile_pool(name="w", bufs=(W_AHEAD + 2) * len(OPERANDS)))
+        sum_pool = stack.enter_context(tc.tile_pool(name="sum", bufs=2 * ITEM_TILES))
+        grouped_pool = stack.enter_context(tc.tile_pool(name="grouped", bufs=3))
+        code_pool = stack.enter_context(tc.tile_pool(name="codes", bufs=3))
+        acc_pool = stack.enter_context(tc.psum_pool(name="acc", bufs=1))
+        bank_pool = stack.enter_context(tc.psum_pool(name="banks", bufs=6))
+        stack.enter_context(tc.manual_schedule())
+
+        h_tiles = {}
+        w_tiles = {}
+        sums = {}
+        banks = {}
+        grouped = {}
+        codes = {}
+        code_scales = {}
+
+        def load_h(c):
+            for i in range(ITEM_TILES):
+                h_tile = h_pool.tile([P, HOPS, CHUNK_K], BF16)
+                nc.sync.dma_start(
+                    out=h_tile[:],
+                    in_=h_sage[i * P : (i + 1) * P, :, c * CHUNK_K : (c + 1) * CHUNK_K],
+                )
+                h_tiles[(c, i)] = h_tile
+
+        def load_words(c):
+            for op in OPERANDS:
+                w_tile = w_pool.tile([P, CHUNK_GROUPS, 2 * COLS], U8, align_bytes=64)
+                nc.sync.dma_start(
+                    out=w_tile[:].bitcast(I32),
+                    in_=words_dram[op][c * CHUNK_GROUPS : (c + 1) * CHUNK_GROUPS]
+                    .rearrange("g p b -> p g b")
+                    .bitcast(I32),
+                )
+                w_tiles[(c, op)] = w_tile
+
+        def load_scales(quarter):
+            g0 = quarter * QUARTER_GROUPS
+            for op in OPERANDS:
+                for b in range(2):
+                    for r in range(4):
+                        nc.sync.dma_start(
+                            out=w_scales[quarter][32 * b + r : P : 64, op, :, :].bitcast(I32),
+                            in_=scales_dram[op][g0 : g0 + QUARTER_GROUPS, 4 * b + r : 16 : 8, :]
+                            .rearrange("g c n -> c g n")
+                            .bitcast(I32),
+                        )
+
+        def add_hops(c):
+            for i in range(ITEM_TILES):
+                hop_sum = sum_pool.tile([P, CHUNK_K], BF16)
+                nc.vector.tensor_add(
+                    out=hop_sum[:], in0=h_tiles[(c, i)][:, 1, :], in1=h_tiles[(c, i)][:, 2, :]
+                )
+                sums[(c, i)] = hop_sum
+
+        def transposes(s):
+            c = s // CHUNK_STEPS
+            for op in (NEIGH, SELF):
+                for i in range(ITEM_TILES):
+                    rows = h_tiles[(c, i)][:, 0, :] if op == SELF else sums[(c, i)][:]
+                    words = rows.bitcast(F32)
+                    bank = bank_pool.tile([P, 2, STEP_GROUPS, P], F32)
+                    for gi in range(STEP_GROUPS):
+                        w0 = ((s % CHUNK_STEPS) * STEP_GROUPS + gi) * GROUP_WORDS
+                        for u in range(2):
+                            nc.tensor.transpose(
+                                bank[:, u, gi, :], words[:, w0 + u : w0 + GROUP_WORDS : 2], ident[:]
+                            )
+                    banks[(s, op, i)] = bank
+
+        def leave_psum(s):
+            neigh_grouped = grouped_pool.tile([P, ITEM_TILES, STEP_GROUPS, P, PACK], BF16, align_bytes=64)
+            self_grouped = grouped_pool.tile([P, ITEM_TILES, STEP_GROUPS, P, PACK], BF16, align_bytes=64)
+            grouped[(s, NEIGH)] = neigh_grouped
+            grouped[(s, SELF)] = self_grouped
+            for i in range(ITEM_TILES):
+                nc.scalar.activation(
+                    out=neigh_grouped[:, i].rearrange("p g r (u e) -> p (g r) u e", e=2),
+                    in_=banks[(s, NEIGH, i)][:]
+                    .bitcast(BF16)
+                    .rearrange("p u g (r e) -> p (g r) u e", e=2),
+                    func=ACT.Copy,
+                    scale=0.5,
+                )
+            for i in range(ITEM_TILES):
+                nc.vector.tensor_copy(
+                    out=self_grouped[:].bitcast(F32)[:, i].rearrange("p g r u -> p (g r) u"),
+                    in_=banks[(s, SELF, i)][:].rearrange("p u g r -> p (g r) u"),
+                )
+
+        def quantise(s):
+            for op in OPERANDS:
+                code = code_pool.tile([P, ITEM_TILES, STEP_GROUPS, P], U32, align_bytes=64, tag="code%d" % op)
+                code_scale = code_pool.tile([P, ITEM_TILES, STEP_GROUPS, P], U8, align_bytes=64, tag="scale%d" % op)
+                nc.vector.quantize_mx(
+                    out=code[:].rearrange("p i g r -> p (i g r)").bitcast(FP8X4),
+                    scales=code_scale[:].rearrange("p i g r -> p (i g r)"),
+                    in_=grouped[(s, op)][:].rearrange("p i g r t -> p (i g r t)"),
+                )
+                codes[(s, op)] = code
+                code_scales[(s, op)] = code_scale
+
+        def passes(s):
+            c = s // CHUNK_STEPS
+            for gi in range(STEP_GROUPS):
+                g = s * STEP_GROUPS + gi
+                for op in OPERANDS:
+                    for i in range(ITEM_TILES):
+                        nc.tensor.matmul_mx(
+                            out=acc[i][:],
+                            lhsT=codes[(s, op)][:, i, gi, :].bitcast(FP8X4),
+                            lhsT_scale=code_scales[(s, op)][:, i, gi, :],
+                            rhs=w_tiles[(c, op)][:, g % CHUNK_GROUPS, :].bitcast(FP4X4),
+                            rhs_scale=w_scales[g // QUARTER_GROUPS][:, op, g % QUARTER_GROUPS, :],
+                            start=(g == 0 and op == OPERANDS[0]),
+                            stop=(g == GROUPS - 1 and op == OPERANDS[-1]),
+                        )
+
+        load_h(0)
+
+        warm = const.tile([P, 1], F32)
+        nc.vector.memset(warm[:], 0.0)
+        nc.scalar.activation(out=warm[:], in_=warm[:], func=ACT.Sigmoid)
+
+        ident = const.tile([P, P], F32)
+        make_identity(nc, ident[:])
+        minus_half = const.tile([P, COL_TILES], F32)
+        nc.vector.memset(minus_half[:], -0.5)
+
+        gb_rows = const.tile([P, P], BF16)
+        nc.vector.memset(gb_rows[:], 0.0)
+        nc.scalar.dma_start(out=gb_rows[0:COL_TILES, :], in_=gamma.rearrange("(j p) -> j p", p=P))
+        nc.scalar.dma_start(
+            out=gb_rows[COL_TILES : 2 * COL_TILES, :], in_=beta.rearrange("(j p) -> j p", p=P)
+        )
+
+        w_scales = []
+        for quarter in range(QUARTERS):
+            plane = const.tile([P, len(OPERANDS), QUARTER_GROUPS, COLS], U8, align_bytes=64, name="plane%d" % quarter)
+            nc.vector.memset(plane[:].bitcast(I32), 0)
+            w_scales.append(plane)
+
+        acc = []
+        for i in range(ITEM_TILES):
+            acc.append(acc_pool.tile([P, COLS], F32, name="acc%d" % i))
+
+        load_scales(0)
+        load_words(0)
+        load_h(1)
+        load_words(1)
+        load_h(2)
+
+        gb_rows_f32 = const.tile([P, P], F32)
+        nc.vector.tensor_copy(out=gb_rows_f32[:], in_=gb_rows[:])
+        gb_bank = bank_pool.tile([P, P], F32, tag="bank")
+        nc.tensor.transpose(gb_bank[:], gb_rows_f32[:], ident[:])
+        gamma_beta = const.tile([P, 2 * COL_TILES], F32)
+        nc.vector.tensor_copy(out=gamma_beta[:], in_=gb_bank[:, 0 : 2 * COL_TILES])
+
+        add_hops(0)
+
+        for s in range(STEPS + 2):
+            if s % CHUNK_STEPS == 0:
+                c = s // CHUNK_STEPS
+                if c + H_AHEAD < CHUNKS:
+                    load_h(c + H_AHEAD)
+                if c + W_AHEAD < CHUNKS:
+                    if (c + W_AHEAD) % QUARTER_CHUNKS == 0:
+                        load_scales((c + W_AHEAD) // QUARTER_CHUNKS)
+                    load_words(c + W_AHEAD)
+                if c + 1 < CHUNKS:
+                    add_hops(c + 1)
+            if s < STEPS:
+                transposes(s)
+                leave_psum(s)
+            if 1 <= s <= STEPS:
+                quantise(s - 1)
+            if s >= 2:
+                passes(s - 2)
+
+        y_rows = []
+        for i in range(ITEM_TILES):
+            y_rows.append(const.tile([P, COLS], F32, name="y_rows%d" % i))
+        nc.vector.tensor_copy(out=y_rows[0][:], in_=acc[0][:])
+        nc.scalar.copy(out=y_rows[1][:], in_=acc[1][:])
+
+        y_cols = []
+        for j in range(COL_TILES):
+            y_cols.append(bank_pool.tile([P, ITEMS], F32, tag="bank", name="y_cols%d" % j))
+        for j in range(COL_TILES):
+            for i in range(ITEM_TILES):
+                nc.tensor.transpose(
+                    y_cols[j][:, i * P : (i + 1) * P], y_rows[i][:, j * P : (j + 1) * P], ident[:]
+                )
+
+        stats = const.tile([P, COL_TILES, 6], F32)
+        mean_var = const.tile([P, COL_TILES, 2], F32)
+        for j in range(COL_TILES):
+            nc.vector.bn_stats(out=stats[:, j, :], in_=y_cols[j][:])
+        for j in range(COL_TILES):
+            nc.vector.bn_aggr(out=mean_var[:, j, :], in_=stats[:, j, :])
+
+        var_eps = const.tile([P, COL_TILES], F32)
+        nc.vector.tensor_scalar_add(out=var_eps[:], in0=mean_var[:, :, 1], scalar1=BN_EPS)
+        rstd = const.tile([P, COL_TILES], F32)
+        nc.gpsimd.tensor_tensor(out=rstd[:], in0=var_eps[:], in1=minus_half[:], op=ALU.pow)
+        gain = const.tile([P, COL_TILES], F32)
+        nc.vector.tensor_mul(out=gain[:], in0=gamma_beta[:, 0:COL_TILES], in1=rstd[:])
+        mean_gain = const.tile([P, COL_TILES], F32)
+        nc.vector.tensor_mul(out=mean_gain[:], in0=mean_var[:, :, 0], in1=gain[:])
+        shift = const.tile([P, COL_TILES], F32)
+        nc.vector.tensor_sub(out=shift[:], in0=gamma_beta[:, COL_TILES : 2 * COL_TILES], in1=mean_gain[:])
+
+        out_cols = const.tile([P, COL_TILES, ITEMS], F32)
+        out_banks = []
+        for i in range(ITEM_TILES):
+            out_banks.append(bank_pool.tile([P, COLS], F32, tag="bank", name="out_bank%d" % i))
+        for j in range(COL_TILES):
+            nc.scalar.activation(
+                out=out_cols[:, j, :],
+                in_=y_cols[j][:],
+                func=ACT.Sigmoid,
+                bias=shift[:, j : j + 1],
+                scale=gain[:, j : j + 1],
+            )
+            for i in range(ITEM_TILES):
+                nc.tensor.transpose(
+                    out_banks[i][:, j * P : (j + 1) * P], out_cols[:, j, i * P : (i + 1) * P], ident[:]
+                )
+
+        out_rows = []
+        for i in range(ITEM_TILES):
+            out_rows.append(const.tile([P, COLS], F32, name="out_rows%d" % i))
+        nc.vector.tensor_copy(out=out_rows[0][:], in_=out_banks[0][:])
+        nc.scalar.copy(out=out_rows[1][:], in_=out_banks[1][:])
+        for i in range(ITEM_TILES):
+            nc.sync.dma_start(out=out[i * P : (i + 1) * P, :], in_=out_rows[i][:])

@@ -16,6 +16,7 @@ ALU = mybir.AluOpType
 P = 128
 PACK = 4
 GROUP_K = P * PACK
+GROUP_WORDS = GROUP_K // 2
 ITEMS = 256
 ITEM_TILES = ITEMS // P
 HOPS = 3
@@ -25,23 +26,21 @@ COL_TILES = COLS // P
 BN_EPS = 1e-5
 
 GROUPS = FEATURES // GROUP_K
-STEP_GROUPS = 2
-STEPS = GROUPS // STEP_GROUPS
 CHUNK_GROUPS = 4
-CHUNK_STEPS = CHUNK_GROUPS // STEP_GROUPS
 CHUNKS = GROUPS // CHUNK_GROUPS
 CHUNK_K = CHUNK_GROUPS * GROUP_K
+STEPS = CHUNKS * ITEM_TILES
+BANK_GROUPS = 2
+STEP_BANKS = CHUNK_GROUPS // BANK_GROUPS
 QUARTER_GROUPS = 8
 QUARTER_CHUNKS = QUARTER_GROUPS // CHUNK_GROUPS
 QUARTERS = GROUPS // QUARTER_GROUPS
-GROUP_WORDS = GROUP_K // 2
 
 SELF = 0
 NEIGH = 1
 OPERANDS = (SELF, NEIGH)
 
-H_AHEAD = 3
-W_AHEAD = 2
+AHEAD = 2
 
 FLOPS = 2 * 2 * ITEMS * FEATURES * COLS
 
@@ -55,9 +54,9 @@ def tile_dogtaitujuanji_pb_k_kernel(
 
     with ExitStack() as stack:
         const = stack.enter_context(tc.tile_pool(name="const", bufs=1))
-        h_pool = stack.enter_context(tc.tile_pool(name="h", bufs=(H_AHEAD + 1) * ITEM_TILES))
-        w_pool = stack.enter_context(tc.tile_pool(name="w", bufs=(W_AHEAD + 2) * len(OPERANDS)))
-        sum_pool = stack.enter_context(tc.tile_pool(name="sum", bufs=2 * ITEM_TILES))
+        h_pool = stack.enter_context(tc.tile_pool(name="h", bufs=(AHEAD + 1) * ITEM_TILES))
+        w_pool = stack.enter_context(tc.tile_pool(name="w", bufs=(AHEAD + 2) * len(OPERANDS)))
+        sum_pool = stack.enter_context(tc.tile_pool(name="sum", bufs=3))
         grouped_pool = stack.enter_context(tc.tile_pool(name="grouped", bufs=3))
         code_pool = stack.enter_context(tc.tile_pool(name="codes", bufs=3))
         acc_pool = stack.enter_context(tc.psum_pool(name="acc", bufs=1))
@@ -79,18 +78,7 @@ def tile_dogtaitujuanji_pb_k_kernel(
                     out=h_tile[:],
                     in_=h_sage[i * P : (i + 1) * P, :, c * CHUNK_K : (c + 1) * CHUNK_K],
                 )
-                h_tiles[(c, i)] = h_tile
-
-        def load_words(c):
-            for op in OPERANDS:
-                w_tile = w_pool.tile([P, CHUNK_GROUPS, 2 * COLS], U8, align_bytes=64)
-                nc.sync.dma_start(
-                    out=w_tile[:].bitcast(I32),
-                    in_=words_dram[op][c * CHUNK_GROUPS : (c + 1) * CHUNK_GROUPS]
-                    .rearrange("g p b -> p g b")
-                    .bitcast(I32),
-                )
-                w_tiles[(c, op)] = w_tile
+                h_tiles[c * ITEM_TILES + i] = h_tile
 
         def load_scales(quarter):
             g0 = quarter * QUARTER_GROUPS
@@ -104,76 +92,88 @@ def tile_dogtaitujuanji_pb_k_kernel(
                             .bitcast(I32),
                         )
 
-        def add_hops(c):
-            for i in range(ITEM_TILES):
-                hop_sum = sum_pool.tile([P, CHUNK_K], BF16)
-                nc.vector.tensor_add(
-                    out=hop_sum[:], in0=h_tiles[(c, i)][:, 1, :], in1=h_tiles[(c, i)][:, 2, :]
+        def load_weights(c):
+            if c % QUARTER_CHUNKS == 0:
+                load_scales(c // QUARTER_CHUNKS)
+            for op in OPERANDS:
+                w_tile = w_pool.tile([P, CHUNK_GROUPS, 2 * COLS], U8, align_bytes=64)
+                nc.sync.dma_start(
+                    out=w_tile[:].bitcast(I32),
+                    in_=words_dram[op][c * CHUNK_GROUPS : (c + 1) * CHUNK_GROUPS]
+                    .rearrange("g p b -> p g b")
+                    .bitcast(I32),
                 )
-                sums[(c, i)] = hop_sum
+                w_tiles[(c, op)] = w_tile
 
-        def transposes(s):
-            c = s // CHUNK_STEPS
-            for op in (NEIGH, SELF):
-                for i in range(ITEM_TILES):
-                    rows = h_tiles[(c, i)][:, 0, :] if op == SELF else sums[(c, i)][:]
-                    words = rows.bitcast(F32)
-                    bank = bank_pool.tile([P, 2, STEP_GROUPS, P], F32)
-                    for gi in range(STEP_GROUPS):
-                        w0 = ((s % CHUNK_STEPS) * STEP_GROUPS + gi) * GROUP_WORDS
+        def add_hops(t):
+            hop_sum = sum_pool.tile([P, CHUNK_K], BF16)
+            nc.vector.tensor_add(out=hop_sum[:], in0=h_tiles[t][:, 1, :], in1=h_tiles[t][:, 2, :])
+            sums[t] = hop_sum
+
+        def transposes(t):
+            for op in OPERANDS:
+                rows = h_tiles[t][:, 0, :] if op == SELF else sums[t][:]
+                words = rows.bitcast(F32)
+                for half in range(STEP_BANKS):
+                    bank = bank_pool.tile([P, 2, BANK_GROUPS, P], F32)
+                    for gi in range(BANK_GROUPS):
+                        w0 = (half * BANK_GROUPS + gi) * GROUP_WORDS
                         for u in range(2):
                             nc.tensor.transpose(
                                 bank[:, u, gi, :], words[:, w0 + u : w0 + GROUP_WORDS : 2], ident[:]
                             )
-                    banks[(s, op, i)] = bank
+                    banks[(t, op, half)] = bank
 
-        def leave_psum(s):
-            neigh_grouped = grouped_pool.tile([P, ITEM_TILES, STEP_GROUPS, P, PACK], BF16, align_bytes=64)
-            self_grouped = grouped_pool.tile([P, ITEM_TILES, STEP_GROUPS, P, PACK], BF16, align_bytes=64)
-            grouped[(s, NEIGH)] = neigh_grouped
-            grouped[(s, SELF)] = self_grouped
-            for i in range(ITEM_TILES):
+        def leave_psum(t):
+            self_grouped = grouped_pool.tile([P, CHUNK_GROUPS, P, PACK], BF16, align_bytes=64)
+            neigh_grouped = grouped_pool.tile([P, CHUNK_GROUPS, P, PACK], BF16, align_bytes=64)
+            grouped[(t, SELF)] = self_grouped
+            grouped[(t, NEIGH)] = neigh_grouped
+            for half in range(STEP_BANKS):
+                g0 = half * BANK_GROUPS
+                nc.vector.tensor_copy(
+                    out=self_grouped[:]
+                    .bitcast(F32)[:, g0 : g0 + BANK_GROUPS]
+                    .rearrange("p g r u -> p (g r) u"),
+                    in_=banks[(t, SELF, half)][:].rearrange("p u g r -> p (g r) u"),
+                )
                 nc.scalar.activation(
-                    out=neigh_grouped[:, i].rearrange("p g r (u e) -> p (g r) u e", e=2),
-                    in_=banks[(s, NEIGH, i)][:]
+                    out=neigh_grouped[:, g0 : g0 + BANK_GROUPS].rearrange(
+                        "p g r (u e) -> p (g r) u e", e=2
+                    ),
+                    in_=banks[(t, NEIGH, half)][:]
                     .bitcast(BF16)
                     .rearrange("p u g (r e) -> p (g r) u e", e=2),
                     func=ACT.Copy,
                     scale=0.5,
                 )
-            for i in range(ITEM_TILES):
-                nc.vector.tensor_copy(
-                    out=self_grouped[:].bitcast(F32)[:, i].rearrange("p g r u -> p (g r) u"),
-                    in_=banks[(s, SELF, i)][:].rearrange("p u g r -> p (g r) u"),
-                )
 
-        def quantise(s):
+        def quantise(t):
             for op in OPERANDS:
-                code = code_pool.tile([P, ITEM_TILES, STEP_GROUPS, P], U32, align_bytes=64, tag="code%d" % op)
-                code_scale = code_pool.tile([P, ITEM_TILES, STEP_GROUPS, P], U8, align_bytes=64, tag="scale%d" % op)
+                code = code_pool.tile([P, CHUNK_GROUPS, P], U32, align_bytes=64, tag="code%d" % op)
+                code_scale = code_pool.tile([P, CHUNK_GROUPS, P], U8, align_bytes=64, tag="scale%d" % op)
                 nc.vector.quantize_mx(
-                    out=code[:].rearrange("p i g r -> p (i g r)").bitcast(FP8X4),
-                    scales=code_scale[:].rearrange("p i g r -> p (i g r)"),
-                    in_=grouped[(s, op)][:].rearrange("p i g r t -> p (i g r t)"),
+                    out=code[:].rearrange("p g r -> p (g r)").bitcast(FP8X4),
+                    scales=code_scale[:].rearrange("p g r -> p (g r)"),
+                    in_=grouped[(t, op)][:].rearrange("p g r t -> p (g r t)"),
                 )
-                codes[(s, op)] = code
-                code_scales[(s, op)] = code_scale
+                codes[(t, op)] = code
+                code_scales[(t, op)] = code_scale
 
-        def passes(s):
-            c = s // CHUNK_STEPS
-            for gi in range(STEP_GROUPS):
-                g = s * STEP_GROUPS + gi
-                for op in OPERANDS:
-                    for i in range(ITEM_TILES):
-                        nc.tensor.matmul_mx(
-                            out=acc[i][:],
-                            lhsT=codes[(s, op)][:, i, gi, :].bitcast(FP8X4),
-                            lhsT_scale=code_scales[(s, op)][:, i, gi, :],
-                            rhs=w_tiles[(c, op)][:, g % CHUNK_GROUPS, :].bitcast(FP4X4),
-                            rhs_scale=w_scales[g // QUARTER_GROUPS][:, op, g % QUARTER_GROUPS, :],
-                            start=(g == 0 and op == OPERANDS[0]),
-                            stop=(g == GROUPS - 1 and op == OPERANDS[-1]),
-                        )
+        def passes(t):
+            c, i = divmod(t, ITEM_TILES)
+            for op in OPERANDS:
+                for gi in range(CHUNK_GROUPS):
+                    g = c * CHUNK_GROUPS + gi
+                    nc.tensor.matmul_mx(
+                        out=acc[i][:],
+                        lhsT=codes[(t, op)][:, gi, :].bitcast(FP8X4),
+                        lhsT_scale=code_scales[(t, op)][:, gi, :],
+                        rhs=w_tiles[(c, op)][:, gi, :].bitcast(FP4X4),
+                        rhs_scale=w_scales[g // QUARTER_GROUPS][:, op, g % QUARTER_GROUPS, :],
+                        start=(g == 0 and op == OPERANDS[0]),
+                        stop=(g == GROUPS - 1 and op == OPERANDS[-1]),
+                    )
 
         load_h(0)
 
@@ -195,7 +195,9 @@ def tile_dogtaitujuanji_pb_k_kernel(
 
         w_scales = []
         for quarter in range(QUARTERS):
-            plane = const.tile([P, len(OPERANDS), QUARTER_GROUPS, COLS], U8, align_bytes=64, name="plane%d" % quarter)
+            plane = const.tile(
+                [P, len(OPERANDS), QUARTER_GROUPS, COLS], U8, align_bytes=64, name="plane%d" % quarter
+            )
             nc.vector.memset(plane[:].bitcast(I32), 0)
             w_scales.append(plane)
 
@@ -203,11 +205,10 @@ def tile_dogtaitujuanji_pb_k_kernel(
         for i in range(ITEM_TILES):
             acc.append(acc_pool.tile([P, COLS], F32, name="acc%d" % i))
 
-        load_scales(0)
-        load_words(0)
-        load_h(1)
-        load_words(1)
-        load_h(2)
+        load_weights(0)
+        for c in range(1, AHEAD):
+            load_h(c)
+            load_weights(c)
 
         gb_rows_f32 = const.tile([P, P], F32)
         nc.vector.tensor_copy(out=gb_rows_f32[:], in_=gb_rows[:])
@@ -216,38 +217,29 @@ def tile_dogtaitujuanji_pb_k_kernel(
         gamma_beta = const.tile([P, 2 * COL_TILES], F32)
         nc.vector.tensor_copy(out=gamma_beta[:], in_=gb_bank[:, 0 : 2 * COL_TILES])
 
-        add_hops(0)
-
-        for s in range(STEPS + 2):
-            if s % CHUNK_STEPS == 0:
-                c = s // CHUNK_STEPS
-                if c + H_AHEAD < CHUNKS:
-                    load_h(c + H_AHEAD)
-                if c + W_AHEAD < CHUNKS:
-                    if (c + W_AHEAD) % QUARTER_CHUNKS == 0:
-                        load_scales((c + W_AHEAD) // QUARTER_CHUNKS)
-                    load_words(c + W_AHEAD)
-                if c + 1 < CHUNKS:
-                    add_hops(c + 1)
-            if s < STEPS:
-                transposes(s)
-                leave_psum(s)
-            if 1 <= s <= STEPS:
-                quantise(s - 1)
-            if s >= 2:
-                passes(s - 2)
+        for t in range(STEPS + 1):
+            if t % ITEM_TILES == 0 and t // ITEM_TILES + AHEAD < CHUNKS:
+                load_h(t // ITEM_TILES + AHEAD)
+                load_weights(t // ITEM_TILES + AHEAD)
+            if t < STEPS:
+                add_hops(t)
+                transposes(t)
+                leave_psum(t)
+                quantise(t)
+            if t >= 1:
+                passes(t - 1)
 
         y_rows = []
         for i in range(ITEM_TILES):
             y_rows.append(const.tile([P, COLS], F32, name="y_rows%d" % i))
-        nc.vector.tensor_copy(out=y_rows[0][:], in_=acc[0][:])
-        nc.scalar.copy(out=y_rows[1][:], in_=acc[1][:])
+        nc.scalar.copy(out=y_rows[0][:], in_=acc[0][:])
+        nc.vector.tensor_copy(out=y_rows[1][:], in_=acc[1][:])
 
         y_cols = []
         for j in range(COL_TILES):
             y_cols.append(bank_pool.tile([P, ITEMS], F32, tag="bank", name="y_cols%d" % j))
-        for j in range(COL_TILES):
-            for i in range(ITEM_TILES):
+        for i in range(ITEM_TILES):
+            for j in range(COL_TILES):
                 nc.tensor.transpose(
                     y_cols[j][:, i * P : (i + 1) * P], y_rows[i][:, j * P : (j + 1) * P], ident[:]
                 )

@@ -32,9 +32,8 @@ CHUNK_K = CHUNK_GROUPS * GROUP_K
 STEPS = CHUNKS * ITEM_TILES
 BANK_GROUPS = 2
 STEP_BANKS = CHUNK_GROUPS // BANK_GROUPS
-QUARTER_GROUPS = 8
-QUARTER_CHUNKS = QUARTER_GROUPS // CHUNK_GROUPS
-QUARTERS = GROUPS // QUARTER_GROUPS
+HALF_GROUPS = 16
+HALVES = GROUPS // HALF_GROUPS
 
 SELF = 0
 NEIGH = 1
@@ -80,21 +79,18 @@ def tile_dogtaitujuanji_pb_k_kernel(
                 )
                 h_tiles[c * ITEM_TILES + i] = h_tile
 
-        def load_scales(quarter):
-            g0 = quarter * QUARTER_GROUPS
+        def load_scales(half):
+            g0 = half * HALF_GROUPS
             for op in OPERANDS:
-                for b in range(2):
-                    for r in range(4):
-                        nc.sync.dma_start(
-                            out=w_scales[quarter][32 * b + r : P : 64, op, :, :].bitcast(I32),
-                            in_=scales_dram[op][g0 : g0 + QUARTER_GROUPS, 4 * b + r : 16 : 8, :]
-                            .rearrange("g c n -> c g n")
-                            .bitcast(I32),
-                        )
+                for r in range(4):
+                    nc.gpsimd.dma_start(
+                        out=w_scales[half][r:P:32, op, :, :].bitcast(F32),
+                        in_=scales_dram[op][g0 : g0 + HALF_GROUPS, r:16:4, :]
+                        .rearrange("g q n -> q g n")
+                        .bitcast(F32),
+                    )
 
         def load_weights(c):
-            if c % QUARTER_CHUNKS == 0:
-                load_scales(c // QUARTER_CHUNKS)
             for op in OPERANDS:
                 w_tile = w_pool.tile([P, CHUNK_GROUPS, 2 * COLS], U8, align_bytes=64)
                 nc.sync.dma_start(
@@ -170,12 +166,21 @@ def tile_dogtaitujuanji_pb_k_kernel(
                         lhsT=codes[(t, op)][:, gi, :].bitcast(FP8X4),
                         lhsT_scale=code_scales[(t, op)][:, gi, :],
                         rhs=w_tiles[(c, op)][:, gi, :].bitcast(FP4X4),
-                        rhs_scale=w_scales[g // QUARTER_GROUPS][:, op, g % QUARTER_GROUPS, :],
+                        rhs_scale=w_scales[g // HALF_GROUPS][:, op, g % HALF_GROUPS, :],
                         start=(g == 0 and op == OPERANDS[0]),
                         stop=(g == GROUPS - 1 and op == OPERANDS[-1]),
                     )
 
-        load_h(0)
+        gb_rows = const.tile([P, P], BF16)
+        nc.vector.memset(gb_rows[:], 0.0)
+        nc.scalar.dma_start(out=gb_rows[0:COL_TILES, :], in_=gamma.rearrange("(j p) -> j p", p=P))
+        nc.scalar.dma_start(
+            out=gb_rows[COL_TILES : 2 * COL_TILES, :], in_=beta.rearrange("(j p) -> j p", p=P)
+        )
+
+        for c in range(AHEAD):
+            load_h(c)
+            load_weights(c)
 
         warm = const.tile([P, 1], F32)
         nc.vector.memset(warm[:], 0.0)
@@ -186,29 +191,18 @@ def tile_dogtaitujuanji_pb_k_kernel(
         minus_half = const.tile([P, COL_TILES], F32)
         nc.vector.memset(minus_half[:], -0.5)
 
-        gb_rows = const.tile([P, P], BF16)
-        nc.vector.memset(gb_rows[:], 0.0)
-        nc.scalar.dma_start(out=gb_rows[0:COL_TILES, :], in_=gamma.rearrange("(j p) -> j p", p=P))
-        nc.scalar.dma_start(
-            out=gb_rows[COL_TILES : 2 * COL_TILES, :], in_=beta.rearrange("(j p) -> j p", p=P)
-        )
-
         w_scales = []
-        for quarter in range(QUARTERS):
+        for half in range(HALVES):
             plane = const.tile(
-                [P, len(OPERANDS), QUARTER_GROUPS, COLS], U8, align_bytes=64, name="plane%d" % quarter
+                [P, len(OPERANDS), HALF_GROUPS, COLS], U8, align_bytes=64, name="plane%d" % half
             )
             nc.vector.memset(plane[:].bitcast(I32), 0)
             w_scales.append(plane)
+            load_scales(half)
 
         acc = []
         for i in range(ITEM_TILES):
             acc.append(acc_pool.tile([P, COLS], F32, name="acc%d" % i))
-
-        load_weights(0)
-        for c in range(1, AHEAD):
-            load_h(c)
-            load_weights(c)
 
         gb_rows_f32 = const.tile([P, P], F32)
         nc.vector.tensor_copy(out=gb_rows_f32[:], in_=gb_rows[:])

@@ -32,8 +32,9 @@ CHUNK_K = CHUNK_GROUPS * GROUP_K
 STEPS = CHUNKS * ITEM_TILES
 BANK_GROUPS = 2
 STEP_BANKS = CHUNK_GROUPS // BANK_GROUPS
-HALF_GROUPS = 16
-HALVES = GROUPS // HALF_GROUPS
+QUARTER_GROUPS = 8
+QUARTER_CHUNKS = QUARTER_GROUPS // CHUNK_GROUPS
+QUARTERS = GROUPS // QUARTER_GROUPS
 
 SELF = 0
 NEIGH = 1
@@ -79,18 +80,21 @@ def tile_dogtaitujuanji_pb_k_kernel(
                 )
                 h_tiles[c * ITEM_TILES + i] = h_tile
 
-        def load_scales(half):
-            g0 = half * HALF_GROUPS
+        def load_scales(quarter):
+            g0 = quarter * QUARTER_GROUPS
             for op in OPERANDS:
-                for r in range(4):
-                    nc.gpsimd.dma_start(
-                        out=w_scales[half][r:P:32, op, :, :].bitcast(F32),
-                        in_=scales_dram[op][g0 : g0 + HALF_GROUPS, r:16:4, :]
-                        .rearrange("g q n -> q g n")
-                        .bitcast(F32),
-                    )
+                for b in range(2):
+                    for r in range(4):
+                        nc.sync.dma_start(
+                            out=w_scales[quarter][32 * b + r : P : 64, op, :, :].bitcast(I32),
+                            in_=scales_dram[op][g0 : g0 + QUARTER_GROUPS, 4 * b + r : 16 : 8, :]
+                            .rearrange("g c n -> c g n")
+                            .bitcast(I32),
+                        )
 
         def load_weights(c):
+            if c % QUARTER_CHUNKS == 0:
+                load_scales(c // QUARTER_CHUNKS)
             for op in OPERANDS:
                 w_tile = w_pool.tile([P, CHUNK_GROUPS, 2 * COLS], U8, align_bytes=64)
                 nc.sync.dma_start(
@@ -106,19 +110,18 @@ def tile_dogtaitujuanji_pb_k_kernel(
             nc.vector.tensor_add(out=hop_sum[:], in0=h_tiles[t][:, 1, :], in1=h_tiles[t][:, 2, :])
             sums[t] = hop_sum
 
-        def transposes(t):
-            for op in OPERANDS:
-                rows = h_tiles[t][:, 0, :] if op == SELF else sums[t][:]
-                words = rows.bitcast(F32)
-                for half in range(STEP_BANKS):
-                    bank = bank_pool.tile([P, 2, BANK_GROUPS, P], F32)
-                    for gi in range(BANK_GROUPS):
-                        w0 = (half * BANK_GROUPS + gi) * GROUP_WORDS
-                        for u in range(2):
-                            nc.tensor.transpose(
-                                bank[:, u, gi, :], words[:, w0 + u : w0 + GROUP_WORDS : 2], ident[:]
-                            )
-                    banks[(t, op, half)] = bank
+        def transposes(t, op):
+            rows = h_tiles[t][:, 0, :] if op == SELF else sums[t][:]
+            words = rows.bitcast(F32)
+            for half in range(STEP_BANKS):
+                bank = bank_pool.tile([P, 2, BANK_GROUPS, P], F32)
+                for gi in range(BANK_GROUPS):
+                    w0 = (half * BANK_GROUPS + gi) * GROUP_WORDS
+                    for u in range(2):
+                        nc.tensor.transpose(
+                            bank[:, u, gi, :], words[:, w0 + u : w0 + GROUP_WORDS : 2], ident[:]
+                        )
+                banks[(t, op, half)] = bank
 
         def leave_psum(t):
             self_grouped = grouped_pool.tile([P, CHUNK_GROUPS, P, PACK], BF16, align_bytes=64)
@@ -156,31 +159,21 @@ def tile_dogtaitujuanji_pb_k_kernel(
                 codes[(t, op)] = code
                 code_scales[(t, op)] = code_scale
 
-        def passes(t):
+        def passes(t, op):
             c, i = divmod(t, ITEM_TILES)
-            for op in OPERANDS:
-                for gi in range(CHUNK_GROUPS):
-                    g = c * CHUNK_GROUPS + gi
-                    nc.tensor.matmul_mx(
-                        out=acc[i][:],
-                        lhsT=codes[(t, op)][:, gi, :].bitcast(FP8X4),
-                        lhsT_scale=code_scales[(t, op)][:, gi, :],
-                        rhs=w_tiles[(c, op)][:, gi, :].bitcast(FP4X4),
-                        rhs_scale=w_scales[g // HALF_GROUPS][:, op, g % HALF_GROUPS, :],
-                        start=(g == 0 and op == OPERANDS[0]),
-                        stop=(g == GROUPS - 1 and op == OPERANDS[-1]),
-                    )
+            for gi in range(CHUNK_GROUPS):
+                g = c * CHUNK_GROUPS + gi
+                nc.tensor.matmul_mx(
+                    out=acc[i][:],
+                    lhsT=codes[(t, op)][:, gi, :].bitcast(FP8X4),
+                    lhsT_scale=code_scales[(t, op)][:, gi, :],
+                    rhs=w_tiles[(c, op)][:, gi, :].bitcast(FP4X4),
+                    rhs_scale=w_scales[g // QUARTER_GROUPS][:, op, g % QUARTER_GROUPS, :],
+                    start=(g == 0 and op == OPERANDS[0]),
+                    stop=(g == GROUPS - 1 and op == OPERANDS[-1]),
+                )
 
-        gb_rows = const.tile([P, P], BF16)
-        nc.vector.memset(gb_rows[:], 0.0)
-        nc.scalar.dma_start(out=gb_rows[0:COL_TILES, :], in_=gamma.rearrange("(j p) -> j p", p=P))
-        nc.scalar.dma_start(
-            out=gb_rows[COL_TILES : 2 * COL_TILES, :], in_=beta.rearrange("(j p) -> j p", p=P)
-        )
-
-        for c in range(AHEAD):
-            load_h(c)
-            load_weights(c)
+        load_h(0)
 
         warm = const.tile([P, 1], F32)
         nc.vector.memset(warm[:], 0.0)
@@ -191,25 +184,32 @@ def tile_dogtaitujuanji_pb_k_kernel(
         minus_half = const.tile([P, COL_TILES], F32)
         nc.vector.memset(minus_half[:], -0.5)
 
+        gb_rows = const.tile([P, P], BF16)
+        nc.vector.memset(gb_rows[:], 0.0)
+        nc.scalar.dma_start(out=gb_rows[0:COL_TILES, :], in_=gamma.rearrange("(j p) -> j p", p=P))
+        nc.scalar.dma_start(
+            out=gb_rows[COL_TILES : 2 * COL_TILES, :], in_=beta.rearrange("(j p) -> j p", p=P)
+        )
+
         w_scales = []
-        for half in range(HALVES):
+        for quarter in range(QUARTERS):
             plane = const.tile(
-                [P, len(OPERANDS), HALF_GROUPS, COLS], U8, align_bytes=64, name="plane%d" % half
+                [P, len(OPERANDS), QUARTER_GROUPS, COLS], U8, align_bytes=64, name="plane%d" % quarter
             )
             nc.vector.memset(plane[:].bitcast(I32), 0)
             w_scales.append(plane)
-            load_scales(half)
 
         acc = []
         for i in range(ITEM_TILES):
             acc.append(acc_pool.tile([P, COLS], F32, name="acc%d" % i))
 
+        load_weights(0)
+        for c in range(1, AHEAD):
+            load_h(c)
+            load_weights(c)
+
         gb_rows_f32 = const.tile([P, P], F32)
         nc.vector.tensor_copy(out=gb_rows_f32[:], in_=gb_rows[:])
-        gb_bank = bank_pool.tile([P, P], F32, tag="bank")
-        nc.tensor.transpose(gb_bank[:], gb_rows_f32[:], ident[:])
-        gamma_beta = const.tile([P, 2 * COL_TILES], F32)
-        nc.vector.tensor_copy(out=gamma_beta[:], in_=gb_bank[:, 0 : 2 * COL_TILES])
 
         for t in range(STEPS + 1):
             if t % ITEM_TILES == 0 and t // ITEM_TILES + AHEAD < CHUNKS:
@@ -217,17 +217,25 @@ def tile_dogtaitujuanji_pb_k_kernel(
                 load_weights(t // ITEM_TILES + AHEAD)
             if t < STEPS:
                 add_hops(t)
-                transposes(t)
+            for op in OPERANDS:
+                if t < STEPS:
+                    transposes(t, op)
+                if t >= 1:
+                    passes(t - 1, op)
+            if t < STEPS:
                 leave_psum(t)
                 quantise(t)
-            if t >= 1:
-                passes(t - 1)
 
         y_rows = []
         for i in range(ITEM_TILES):
             y_rows.append(const.tile([P, COLS], F32, name="y_rows%d" % i))
         nc.scalar.copy(out=y_rows[0][:], in_=acc[0][:])
         nc.vector.tensor_copy(out=y_rows[1][:], in_=acc[1][:])
+
+        gb_bank = bank_pool.tile([P, P], F32, tag="bank")
+        nc.tensor.transpose(gb_bank[:], gb_rows_f32[:], ident[:])
+        gamma_beta = const.tile([P, 2 * COL_TILES], F32)
+        nc.vector.tensor_copy(out=gamma_beta[:], in_=gb_bank[:, 0 : 2 * COL_TILES])
 
         y_cols = []
         for j in range(COL_TILES):

@@ -33,8 +33,9 @@ STEPS = CHUNKS * ITEM_TILES
 BANK_GROUPS = 2
 STEP_BANKS = CHUNK_GROUPS // BANK_GROUPS
 QUARTER_GROUPS = 8
-QUARTER_CHUNKS = QUARTER_GROUPS // CHUNK_GROUPS
 QUARTERS = GROUPS // QUARTER_GROUPS
+CHUNK_LOADS = ITEM_TILES + 2
+QUARTER_LOADS = CHUNK_LOADS * QUARTER_GROUPS // CHUNK_GROUPS
 
 SELF = 0
 NEIGH = 1
@@ -79,22 +80,24 @@ def tile_dogtaitujuanji_pb_k_kernel(
                     in_=h_sage[i * P : (i + 1) * P, :, c * CHUNK_K : (c + 1) * CHUNK_K],
                 )
                 h_tiles[c * ITEM_TILES + i] = h_tile
+                load_scale_rows_behind(c * CHUNK_LOADS + i)
 
-        def load_scales(quarter):
+        def load_scale_rows(quarter, n):
+            op, r = divmod(n, 4)
             g0 = quarter * QUARTER_GROUPS
-            for op in OPERANDS:
-                for b in range(2):
-                    for r in range(4):
-                        nc.sync.dma_start(
-                            out=w_scales[quarter][32 * b + r : P : 64, op, :, :].bitcast(I32),
-                            in_=scales_dram[op][g0 : g0 + QUARTER_GROUPS, 4 * b + r : 16 : 8, :]
-                            .rearrange("g c n -> c g n")
-                            .bitcast(I32),
-                        )
+            nc.sync.dma_start(
+                out=w_scales[quarter][r:P:32, op, :, :].bitcast(I32),
+                in_=scales_dram[op][g0 : g0 + QUARTER_GROUPS, r:16:4, :]
+                .rearrange("g q n -> q g n")
+                .bitcast(I32),
+            )
+
+        def load_scale_rows_behind(load):
+            quarter = load // QUARTER_LOADS + 1
+            if quarter < QUARTERS:
+                load_scale_rows(quarter, load % QUARTER_LOADS)
 
         def load_weights(c):
-            if c % QUARTER_CHUNKS == 0:
-                load_scales(c // QUARTER_CHUNKS)
             for op in OPERANDS:
                 w_tile = w_pool.tile([P, CHUNK_GROUPS, 2 * COLS], U8, align_bytes=64)
                 nc.sync.dma_start(
@@ -104,24 +107,26 @@ def tile_dogtaitujuanji_pb_k_kernel(
                     .bitcast(I32),
                 )
                 w_tiles[(c, op)] = w_tile
+                load_scale_rows_behind(c * CHUNK_LOADS + ITEM_TILES + op)
 
         def add_hops(t):
             hop_sum = sum_pool.tile([P, CHUNK_K], BF16)
             nc.vector.tensor_add(out=hop_sum[:], in0=h_tiles[t][:, 1, :], in1=h_tiles[t][:, 2, :])
             sums[t] = hop_sum
 
-        def transposes(t, op):
-            rows = h_tiles[t][:, 0, :] if op == SELF else sums[t][:]
-            words = rows.bitcast(F32)
-            for half in range(STEP_BANKS):
-                bank = bank_pool.tile([P, 2, BANK_GROUPS, P], F32)
-                for gi in range(BANK_GROUPS):
-                    w0 = (half * BANK_GROUPS + gi) * GROUP_WORDS
-                    for u in range(2):
-                        nc.tensor.transpose(
-                            bank[:, u, gi, :], words[:, w0 + u : w0 + GROUP_WORDS : 2], ident[:]
-                        )
-                banks[(t, op, half)] = bank
+        def transposes(t):
+            for op in OPERANDS:
+                rows = h_tiles[t][:, 0, :] if op == SELF else sums[t][:]
+                words = rows.bitcast(F32)
+                for half in range(STEP_BANKS):
+                    bank = bank_pool.tile([P, 2, BANK_GROUPS, P], F32)
+                    for gi in range(BANK_GROUPS):
+                        w0 = (half * BANK_GROUPS + gi) * GROUP_WORDS
+                        for u in range(2):
+                            nc.tensor.transpose(
+                                bank[:, u, gi, :], words[:, w0 + u : w0 + GROUP_WORDS : 2], ident[:]
+                            )
+                    banks[(t, op, half)] = bank
 
         def leave_psum(t):
             self_grouped = grouped_pool.tile([P, CHUNK_GROUPS, P, PACK], BF16, align_bytes=64)
@@ -147,40 +152,55 @@ def tile_dogtaitujuanji_pb_k_kernel(
                     scale=0.5,
                 )
 
-        def quantise(t):
-            for op in OPERANDS:
-                code = code_pool.tile([P, CHUNK_GROUPS, P], U32, align_bytes=64, tag="code%d" % op)
-                code_scale = code_pool.tile([P, CHUNK_GROUPS, P], U8, align_bytes=64, tag="scale%d" % op)
-                nc.vector.quantize_mx(
-                    out=code[:].rearrange("p g r -> p (g r)").bitcast(FP8X4),
-                    scales=code_scale[:].rearrange("p g r -> p (g r)"),
-                    in_=grouped[(t, op)][:].rearrange("p g r t -> p (g r t)"),
-                )
-                codes[(t, op)] = code
-                code_scales[(t, op)] = code_scale
+        def quantise(t, op):
+            code = code_pool.tile([P, CHUNK_GROUPS, P], U32, align_bytes=64, tag="code%d" % op)
+            code_scale = code_pool.tile([P, CHUNK_GROUPS, P], U8, align_bytes=64, tag="scale%d" % op)
+            nc.vector.quantize_mx(
+                out=code[:].rearrange("p g r -> p (g r)").bitcast(FP8X4),
+                scales=code_scale[:].rearrange("p g r -> p (g r)"),
+                in_=grouped[(t, op)][:].rearrange("p g r t -> p (g r t)"),
+            )
+            codes[(t, op)] = code
+            code_scales[(t, op)] = code_scale
 
-        def passes(t, op):
+        def passes(t):
             c, i = divmod(t, ITEM_TILES)
-            for gi in range(CHUNK_GROUPS):
-                g = c * CHUNK_GROUPS + gi
-                nc.tensor.matmul_mx(
-                    out=acc[i][:],
-                    lhsT=codes[(t, op)][:, gi, :].bitcast(FP8X4),
-                    lhsT_scale=code_scales[(t, op)][:, gi, :],
-                    rhs=w_tiles[(c, op)][:, gi, :].bitcast(FP4X4),
-                    rhs_scale=w_scales[g // QUARTER_GROUPS][:, op, g % QUARTER_GROUPS, :],
-                    start=(g == 0 and op == OPERANDS[0]),
-                    stop=(g == GROUPS - 1 and op == OPERANDS[-1]),
-                )
+            for op in OPERANDS:
+                for gi in range(CHUNK_GROUPS):
+                    g = c * CHUNK_GROUPS + gi
+                    nc.tensor.matmul_mx(
+                        out=acc[i][:],
+                        lhsT=codes[(t, op)][:, gi, :].bitcast(FP8X4),
+                        lhsT_scale=code_scales[(t, op)][:, gi, :],
+                        rhs=w_tiles[(c, op)][:, gi, :].bitcast(FP4X4),
+                        rhs_scale=w_scales[g // QUARTER_GROUPS][:, op, g % QUARTER_GROUPS, :],
+                        start=(g == 0 and op == OPERANDS[0]),
+                        stop=(g == GROUPS - 1 and op == OPERANDS[-1]),
+                    )
+
+        w_scales = []
+        for quarter in range(QUARTERS):
+            plane = const.tile(
+                [P, len(OPERANDS), QUARTER_GROUPS, COLS], U8, align_bytes=64, name="plane%d" % quarter
+            )
+            nc.vector.memset(plane[:].bitcast(I32), 0)
+            w_scales.append(plane)
 
         load_h(0)
+        for n in range(QUARTER_LOADS):
+            load_scale_rows(0, n)
+        load_weights(0)
+        for c in range(1, AHEAD):
+            load_h(c)
+            load_weights(c)
+
+        ident = const.tile([P, P], F32)
+        make_identity(nc, ident[:])
 
         warm = const.tile([P, 1], F32)
         nc.vector.memset(warm[:], 0.0)
         nc.scalar.activation(out=warm[:], in_=warm[:], func=ACT.Sigmoid)
 
-        ident = const.tile([P, P], F32)
-        make_identity(nc, ident[:])
         minus_half = const.tile([P, COL_TILES], F32)
         nc.vector.memset(minus_half[:], -0.5)
 
@@ -191,40 +211,27 @@ def tile_dogtaitujuanji_pb_k_kernel(
             out=gb_rows[COL_TILES : 2 * COL_TILES, :], in_=beta.rearrange("(j p) -> j p", p=P)
         )
 
-        w_scales = []
-        for quarter in range(QUARTERS):
-            plane = const.tile(
-                [P, len(OPERANDS), QUARTER_GROUPS, COLS], U8, align_bytes=64, name="plane%d" % quarter
-            )
-            nc.vector.memset(plane[:].bitcast(I32), 0)
-            w_scales.append(plane)
-
         acc = []
         for i in range(ITEM_TILES):
             acc.append(acc_pool.tile([P, COLS], F32, name="acc%d" % i))
 
-        load_weights(0)
-        for c in range(1, AHEAD):
-            load_h(c)
-            load_weights(c)
-
-        gb_rows_f32 = const.tile([P, P], F32)
-        nc.vector.tensor_copy(out=gb_rows_f32[:], in_=gb_rows[:])
-
+        add_hops(0)
         for t in range(STEPS + 1):
             if t % ITEM_TILES == 0 and t // ITEM_TILES + AHEAD < CHUNKS:
                 load_h(t // ITEM_TILES + AHEAD)
                 load_weights(t // ITEM_TILES + AHEAD)
             if t < STEPS:
-                add_hops(t)
-            for op in OPERANDS:
-                if t < STEPS:
-                    transposes(t, op)
-                if t >= 1:
-                    passes(t - 1, op)
-            if t < STEPS:
+                transposes(t)
                 leave_psum(t)
-                quantise(t)
+                quantise(t, SELF)
+                if t + 1 < STEPS:
+                    add_hops(t + 1)
+                quantise(t, NEIGH)
+            if t >= 1:
+                passes(t - 1)
+
+        gb_rows_f32 = const.tile([P, P], F32)
+        nc.vector.tensor_copy(out=gb_rows_f32[:], in_=gb_rows[:])
 
         y_rows = []
         for i in range(ITEM_TILES):

@@ -34,8 +34,9 @@ BANK_GROUPS = 2
 STEP_BANKS = CHUNK_GROUPS // BANK_GROUPS
 QUARTER_GROUPS = 8
 QUARTERS = GROUPS // QUARTER_GROUPS
+QUARTER_DMAS = 8
 CHUNK_LOADS = ITEM_TILES + 2
-QUARTER_LOADS = CHUNK_LOADS * QUARTER_GROUPS // CHUNK_GROUPS
+SMALL_PER_LARGE = 2
 
 SELF = 0
 NEIGH = 1
@@ -93,9 +94,9 @@ def tile_dogtaitujuanji_pb_k_kernel(
             )
 
         def load_scale_rows_behind(load):
-            quarter = load // QUARTER_LOADS + 1
-            if quarter < QUARTERS:
-                load_scale_rows(quarter, load % QUARTER_LOADS)
+            for m in range(SMALL_PER_LARGE * load, SMALL_PER_LARGE * (load + 1)):
+                if m < QUARTERS * QUARTER_DMAS:
+                    load_scale_rows(m // QUARTER_DMAS, m % QUARTER_DMAS)
 
         def load_weights(c):
             for op in OPERANDS:
@@ -186,11 +187,7 @@ def tile_dogtaitujuanji_pb_k_kernel(
             nc.vector.memset(plane[:].bitcast(I32), 0)
             w_scales.append(plane)
 
-        load_h(0)
-        for n in range(QUARTER_LOADS):
-            load_scale_rows(0, n)
-        load_weights(0)
-        for c in range(1, AHEAD):
+        for c in range(AHEAD):
             load_h(c)
             load_weights(c)
 
@@ -236,8 +233,8 @@ def tile_dogtaitujuanji_pb_k_kernel(
         y_rows = []
         for i in range(ITEM_TILES):
             y_rows.append(const.tile([P, COLS], F32, name="y_rows%d" % i))
-        nc.scalar.copy(out=y_rows[0][:], in_=acc[0][:])
-        nc.vector.tensor_copy(out=y_rows[1][:], in_=acc[1][:])
+        for i in range(ITEM_TILES):
+            nc.scalar.copy(out=y_rows[i][:], in_=acc[i][:])
 
         gb_bank = bank_pool.tile([P, P], F32, tag="bank")
         nc.tensor.transpose(gb_bank[:], gb_rows_f32[:], ident[:])
@@ -247,27 +244,30 @@ def tile_dogtaitujuanji_pb_k_kernel(
         y_cols = []
         for j in range(COL_TILES):
             y_cols.append(bank_pool.tile([P, ITEMS], F32, tag="bank", name="y_cols%d" % j))
+        stats = const.tile([P, COL_TILES, ITEM_TILES, 6], F32)
         for i in range(ITEM_TILES):
             for j in range(COL_TILES):
                 nc.tensor.transpose(
                     y_cols[j][:, i * P : (i + 1) * P], y_rows[i][:, j * P : (j + 1) * P], ident[:]
                 )
-
-        stats = const.tile([P, COL_TILES, 6], F32)
+            for j in range(COL_TILES):
+                nc.vector.bn_stats(out=stats[:, j, i, :], in_=y_cols[j][:, i * P : (i + 1) * P])
         mean_var = const.tile([P, COL_TILES, 2], F32)
         for j in range(COL_TILES):
-            nc.vector.bn_stats(out=stats[:, j, :], in_=y_cols[j][:])
-        for j in range(COL_TILES):
-            nc.vector.bn_aggr(out=mean_var[:, j, :], in_=stats[:, j, :])
+            nc.vector.bn_aggr(
+                out=mean_var[:, j, :], in_=stats[:, j, :, :].rearrange("p i s -> p (i s)")
+            )
 
         var_eps = const.tile([P, COL_TILES], F32)
         nc.vector.tensor_scalar_add(out=var_eps[:], in0=mean_var[:, :, 1], scalar1=BN_EPS)
         rstd = const.tile([P, COL_TILES], F32)
         nc.gpsimd.tensor_tensor(out=rstd[:], in0=var_eps[:], in1=minus_half[:], op=ALU.pow)
+        mean_gamma = const.tile([P, COL_TILES], F32)
+        nc.vector.tensor_mul(out=mean_gamma[:], in0=mean_var[:, :, 0], in1=gamma_beta[:, 0:COL_TILES])
+        mean_gain = const.tile([P, COL_TILES], F32)
+        nc.vector.tensor_mul(out=mean_gain[:], in0=mean_gamma[:], in1=rstd[:])
         gain = const.tile([P, COL_TILES], F32)
         nc.vector.tensor_mul(out=gain[:], in0=gamma_beta[:, 0:COL_TILES], in1=rstd[:])
-        mean_gain = const.tile([P, COL_TILES], F32)
-        nc.vector.tensor_mul(out=mean_gain[:], in0=mean_var[:, :, 0], in1=gain[:])
         shift = const.tile([P, COL_TILES], F32)
         nc.vector.tensor_sub(out=shift[:], in0=gamma_beta[:, COL_TILES : 2 * COL_TILES], in1=mean_gain[:])
 

@@ -35,8 +35,6 @@ STEP_BANKS = CHUNK_GROUPS // BANK_GROUPS
 QUARTER_GROUPS = 8
 QUARTERS = GROUPS // QUARTER_GROUPS
 QUARTER_DMAS = 8
-CHUNK_LOADS = ITEM_TILES + 2
-SMALL_PER_LARGE = 2
 
 SELF = 0
 NEIGH = 1
@@ -81,7 +79,6 @@ def tile_dogtaitujuanji_pb_k_kernel(
                     in_=h_sage[i * P : (i + 1) * P, :, c * CHUNK_K : (c + 1) * CHUNK_K],
                 )
                 h_tiles[c * ITEM_TILES + i] = h_tile
-                load_scale_rows_behind(c * CHUNK_LOADS + i)
 
         def load_scale_rows(quarter, n):
             op, r = divmod(n, 4)
@@ -93,11 +90,6 @@ def tile_dogtaitujuanji_pb_k_kernel(
                 .bitcast(I32),
             )
 
-        def load_scale_rows_behind(load):
-            for m in range(SMALL_PER_LARGE * load, SMALL_PER_LARGE * (load + 1)):
-                if m < QUARTERS * QUARTER_DMAS:
-                    load_scale_rows(m // QUARTER_DMAS, m % QUARTER_DMAS)
-
         def load_weights(c):
             for op in OPERANDS:
                 w_tile = w_pool.tile([P, CHUNK_GROUPS, 2 * COLS], U8, align_bytes=64)
@@ -108,7 +100,6 @@ def tile_dogtaitujuanji_pb_k_kernel(
                     .bitcast(I32),
                 )
                 w_tiles[(c, op)] = w_tile
-                load_scale_rows_behind(c * CHUNK_LOADS + ITEM_TILES + op)
 
         def add_hops(t):
             hop_sum = sum_pool.tile([P, CHUNK_K], BF16)
@@ -186,6 +177,10 @@ def tile_dogtaitujuanji_pb_k_kernel(
             )
             nc.vector.memset(plane[:].bitcast(I32), 0)
             w_scales.append(plane)
+
+        for quarter in range(QUARTERS):
+            for n in range(QUARTER_DMAS):
+                load_scale_rows(quarter, n)
 
         for c in range(AHEAD):
             load_h(c)

@@ -16,7 +16,6 @@ ALU = mybir.AluOpType
 P = 128
 PACK = 4
 GROUP_K = P * PACK
-GROUP_WORDS = GROUP_K // 2
 ITEMS = 256
 ITEM_TILES = ITEMS // P
 HOPS = 3
@@ -56,7 +55,7 @@ def tile_dogtaitujuanji_pb_k_kernel(
         const = stack.enter_context(tc.tile_pool(name="const", bufs=1))
         h_pool = stack.enter_context(tc.tile_pool(name="h", bufs=(AHEAD + 1) * ITEM_TILES))
         w_pool = stack.enter_context(tc.tile_pool(name="w", bufs=(AHEAD + 2) * len(OPERANDS)))
-        sum_pool = stack.enter_context(tc.tile_pool(name="sum", bufs=3))
+        split_pool = stack.enter_context(tc.tile_pool(name="split", bufs=3))
         grouped_pool = stack.enter_context(tc.tile_pool(name="grouped", bufs=3))
         code_pool = stack.enter_context(tc.tile_pool(name="codes", bufs=3))
         acc_pool = stack.enter_context(tc.psum_pool(name="acc", bufs=1))
@@ -65,7 +64,7 @@ def tile_dogtaitujuanji_pb_k_kernel(
 
         h_tiles = {}
         w_tiles = {}
-        sums = {}
+        split_words = {}
         banks = {}
         grouped = {}
         codes = {}
@@ -102,22 +101,31 @@ def tile_dogtaitujuanji_pb_k_kernel(
                 w_tiles[(c, op)] = w_tile
 
         def add_hops(t):
-            hop_sum = sum_pool.tile([P, CHUNK_K], BF16)
-            nc.vector.tensor_add(out=hop_sum[:], in0=h_tiles[t][:, 1, :], in1=h_tiles[t][:, 2, :])
-            sums[t] = hop_sum
+            hop_sum = split_pool.tile([P, 2, CHUNK_K // PACK, 2], BF16)
+            nc.vector.tensor_add(
+                out=hop_sum[:],
+                in0=h_tiles[t][:, 1, :].rearrange("p (w u e) -> p u w e", u=2, e=2),
+                in1=h_tiles[t][:, 2, :].rearrange("p (w u e) -> p u w e", u=2, e=2),
+            )
+            split_words[(t, NEIGH)] = hop_sum[:].rearrange("p u w e -> p u (w e)").bitcast(F32)
+
+        def split_self(t):
+            self_split = split_pool.tile([P, 2, CHUNK_K // PACK], F32)
+            nc.scalar.copy(
+                out=self_split[:],
+                in_=h_tiles[t][:, 0, :].bitcast(F32).rearrange("p (w u) -> p u w", u=2),
+            )
+            split_words[(t, SELF)] = self_split[:]
 
         def transposes(t):
-            for op in OPERANDS:
-                rows = h_tiles[t][:, 0, :] if op == SELF else sums[t][:]
-                words = rows.bitcast(F32)
+            for op in (NEIGH, SELF):
+                words = split_words[(t, op)]
                 for half in range(STEP_BANKS):
                     bank = bank_pool.tile([P, 2, BANK_GROUPS, P], F32)
                     for gi in range(BANK_GROUPS):
-                        w0 = (half * BANK_GROUPS + gi) * GROUP_WORDS
+                        w0 = (half * BANK_GROUPS + gi) * P
                         for u in range(2):
-                            nc.tensor.transpose(
-                                bank[:, u, gi, :], words[:, w0 + u : w0 + GROUP_WORDS : 2], ident[:]
-                            )
+                            nc.tensor.transpose(bank[:, u, gi, :], words[:, u, w0 : w0 + P], ident[:])
                     banks[(t, op, half)] = bank
 
         def leave_psum(t):
@@ -208,6 +216,7 @@ def tile_dogtaitujuanji_pb_k_kernel(
             acc.append(acc_pool.tile([P, COLS], F32, name="acc%d" % i))
 
         add_hops(0)
+        split_self(0)
         for t in range(STEPS + 1):
             if t % ITEM_TILES == 0 and t // ITEM_TILES + AHEAD < CHUNKS:
                 load_h(t // ITEM_TILES + AHEAD)
@@ -215,9 +224,10 @@ def tile_dogtaitujuanji_pb_k_kernel(
             if t < STEPS:
                 transposes(t)
                 leave_psum(t)
-                quantise(t, SELF)
                 if t + 1 < STEPS:
                     add_hops(t + 1)
+                    split_self(t + 1)
+                quantise(t, SELF)
                 quantise(t, NEIGH)
             if t >= 1:
                 passes(t - 1)

@@ -22,15 +22,12 @@ HOPS = 3
 FEATURES = 16384
 COLS = 512
 COL_TILES = COLS // P
+HALVES = 2
+PAIR = COL_TILES // HALVES
 BN_EPS = 1e-5
 
 GROUPS = FEATURES // GROUP_K
-CHUNK_GROUPS = 4
-CHUNKS = GROUPS // CHUNK_GROUPS
-CHUNK_K = CHUNK_GROUPS * GROUP_K
-STEPS = CHUNKS * ITEM_TILES
 BANK_GROUPS = 2
-STEP_BANKS = CHUNK_GROUPS // BANK_GROUPS
 QUARTER_GROUPS = 8
 QUARTERS = GROUPS // QUARTER_GROUPS
 QUARTER_DMAS = 8
@@ -39,9 +36,12 @@ SELF = 0
 NEIGH = 1
 OPERANDS = (SELF, NEIGH)
 
-AHEAD = 2
-
 FLOPS = 2 * 2 * ITEMS * FEATURES * COLS
+
+LOAD_PLAN = (4, 4, 4, 4, 4, 4, 4, 4)
+STEP_GROUPS = 4
+H_BUFS = 6
+W_BUFS = 8
 
 
 def tile_dogtaitujuanji_pb_k_kernel(
@@ -51,15 +51,32 @@ def tile_dogtaitujuanji_pb_k_kernel(
     words_dram = (w2b_words, w1b_words)
     scales_dram = (w2b_scales, w1b_scales)
 
+    chunks = []
+    for groups in LOAD_PLAN:
+        chunks.append((sum(n for g, n in chunks), groups))
+    steps = []
+    for c, (c0, groups) in enumerate(chunks):
+        for i in range(ITEM_TILES):
+            for g0 in range(c0, c0 + groups, STEP_GROUPS):
+                steps.append((c, i, g0, min(STEP_GROUPS, c0 + groups - g0)))
+    n_steps = len(steps)
+    first_step = [min(s for s in range(n_steps) if steps[s][1] == i) for i in range(ITEM_TILES)]
+    last_step = [max(s for s in range(n_steps) if steps[s][1] == i) for i in range(ITEM_TILES)]
+    last_h_use = {}
+    last_w_use = {}
+    for s, (c, i, g0, groups) in enumerate(steps):
+        last_h_use[(c, i)] = s
+        last_w_use[c] = s
+
     with ExitStack() as stack:
         const = stack.enter_context(tc.tile_pool(name="const", bufs=1))
-        h_pool = stack.enter_context(tc.tile_pool(name="h", bufs=(AHEAD + 1) * ITEM_TILES))
-        w_pool = stack.enter_context(tc.tile_pool(name="w", bufs=(AHEAD + 2) * len(OPERANDS)))
+        h_pool = stack.enter_context(tc.tile_pool(name="h", bufs=H_BUFS))
+        w_pool = stack.enter_context(tc.tile_pool(name="w", bufs=W_BUFS))
         split_pool = stack.enter_context(tc.tile_pool(name="split", bufs=3))
         grouped_pool = stack.enter_context(tc.tile_pool(name="grouped", bufs=3))
         code_pool = stack.enter_context(tc.tile_pool(name="codes", bufs=3))
         acc_pool = stack.enter_context(tc.psum_pool(name="acc", bufs=1))
-        bank_pool = stack.enter_context(tc.psum_pool(name="banks", bufs=6))
+        bank_pool = stack.enter_context(tc.psum_pool(name="banks", bufs=4))
         stack.enter_context(tc.manual_schedule())
 
         h_tiles = {}
@@ -69,15 +86,18 @@ def tile_dogtaitujuanji_pb_k_kernel(
         grouped = {}
         codes = {}
         code_scales = {}
+        live = {"h": 0, "w": 0, "issued": 0}
+        pending = []
 
-        def load_h(c):
-            for i in range(ITEM_TILES):
-                h_tile = h_pool.tile([P, HOPS, CHUNK_K], BF16)
-                nc.sync.dma_start(
-                    out=h_tile[:],
-                    in_=h_sage[i * P : (i + 1) * P, :, c * CHUNK_K : (c + 1) * CHUNK_K],
-                )
-                h_tiles[c * ITEM_TILES + i] = h_tile
+        def load_h(c, i):
+            c0, groups = chunks[c]
+            h_tile = h_pool.tile([P, HOPS, groups * GROUP_K], BF16)
+            queue = nc.sync if i == 0 else nc.sync
+            queue.dma_start(
+                out=h_tile[:],
+                in_=h_sage[i * P : (i + 1) * P, :, c0 * GROUP_K : (c0 + groups) * GROUP_K],
+            )
+            h_tiles[(c, i)] = h_tile
 
         def load_scale_rows(quarter, n):
             op, r = divmod(n, 4)
@@ -89,94 +109,114 @@ def tile_dogtaitujuanji_pb_k_kernel(
                 .bitcast(I32),
             )
 
-        def load_weights(c):
-            for op in OPERANDS:
-                w_tile = w_pool.tile([P, CHUNK_GROUPS, 2 * COLS], U8, align_bytes=64)
-                nc.sync.dma_start(
-                    out=w_tile[:].bitcast(I32),
-                    in_=words_dram[op][c * CHUNK_GROUPS : (c + 1) * CHUNK_GROUPS]
-                    .rearrange("g p b -> p g b")
-                    .bitcast(I32),
-                )
-                w_tiles[(c, op)] = w_tile
+        def load_weights(c, op):
+            c0, groups = chunks[c]
+            w_tile = w_pool.tile([P, groups, 2 * COLS], U8, align_bytes=64)
+            nc.sync.dma_start(
+                out=w_tile[:].bitcast(I32),
+                in_=words_dram[op][c0 : c0 + groups].rearrange("g p b -> p g b").bitcast(I32),
+            )
+            w_tiles[(c, op)] = w_tile
 
-        def add_hops(t):
-            hop_sum = split_pool.tile([P, 2, CHUNK_K // PACK, 2], BF16)
+        def issue_loads():
+            while live["issued"] < len(pending):
+                kind, c, x = pending[live["issued"]]
+                if kind == "h":
+                    if live["h"] == H_BUFS:
+                        return
+                    load_h(c, x)
+                    live["h"] = live["h"] + 1
+                elif kind == "w":
+                    if live["w"] == W_BUFS:
+                        return
+                    load_weights(c, x)
+                    live["w"] = live["w"] + 1
+                else:
+                    for quarter in range(QUARTERS):
+                        for n in range(QUARTER_DMAS):
+                            load_scale_rows(quarter, n)
+                live["issued"] = live["issued"] + 1
+
+        def add_hops(s):
+            c, i, g0, groups = steps[s]
+            k0 = (g0 - chunks[c][0]) * GROUP_K
+            k1 = k0 + groups * GROUP_K
+            hop_sum = split_pool.tile([P, 2, groups * P, 2], BF16)
             nc.vector.tensor_add(
                 out=hop_sum[:],
-                in0=h_tiles[t][:, 1, :].rearrange("p (w u e) -> p u w e", u=2, e=2),
-                in1=h_tiles[t][:, 2, :].rearrange("p (w u e) -> p u w e", u=2, e=2),
+                in0=h_tiles[(c, i)][:, 1, k0:k1].rearrange("p (w u e) -> p u w e", u=2, e=2),
+                in1=h_tiles[(c, i)][:, 2, k0:k1].rearrange("p (w u e) -> p u w e", u=2, e=2),
             )
-            split_words[(t, NEIGH)] = hop_sum[:].rearrange("p u w e -> p u (w e)").bitcast(F32)
+            split_words[(s, NEIGH)] = hop_sum[:].rearrange("p u w e -> p u (w e)").bitcast(F32)
+            if last_h_use[(c, i)] == s:
+                live["h"] = live["h"] - 1
 
-        def split_self(t):
-            self_split = split_pool.tile([P, 2, CHUNK_K // PACK], F32)
-            nc.scalar.copy(
+        def split_self(s):
+            c, i, g0, groups = steps[s]
+            k0 = (g0 - chunks[c][0]) * GROUP_K
+            k1 = k0 + groups * GROUP_K
+            self_split = split_pool.tile([P, 2, groups * P], F32)
+            nc.vector.tensor_copy(
                 out=self_split[:],
-                in_=h_tiles[t][:, 0, :].bitcast(F32).rearrange("p (w u) -> p u w", u=2),
+                in_=h_tiles[(c, i)][:, 0, k0:k1].bitcast(F32).rearrange("p (w u) -> p u w", u=2),
             )
-            split_words[(t, SELF)] = self_split[:]
+            split_words[(s, SELF)] = self_split[:]
 
-        def transposes(t):
-            for op in (NEIGH, SELF):
-                words = split_words[(t, op)]
-                for half in range(STEP_BANKS):
-                    bank = bank_pool.tile([P, 2, BANK_GROUPS, P], F32)
-                    for gi in range(BANK_GROUPS):
-                        w0 = (half * BANK_GROUPS + gi) * P
+        def transposes(s):
+            groups = steps[s][3]
+            for op in OPERANDS:
+                words = split_words[(s, op)]
+                for b0 in range(0, groups, BANK_GROUPS):
+                    in_bank = min(BANK_GROUPS, groups - b0)
+                    bank = bank_pool.tile([P, 2, in_bank, P], F32)
+                    for gi in range(in_bank):
+                        w0 = (b0 + gi) * P
                         for u in range(2):
                             nc.tensor.transpose(bank[:, u, gi, :], words[:, u, w0 : w0 + P], ident[:])
-                    banks[(t, op, half)] = bank
+                    banks[(s, op, b0)] = bank
 
-        def leave_psum(t):
-            self_grouped = grouped_pool.tile([P, CHUNK_GROUPS, P, PACK], BF16, align_bytes=64)
-            neigh_grouped = grouped_pool.tile([P, CHUNK_GROUPS, P, PACK], BF16, align_bytes=64)
-            grouped[(t, SELF)] = self_grouped
-            grouped[(t, NEIGH)] = neigh_grouped
-            for half in range(STEP_BANKS):
-                g0 = half * BANK_GROUPS
-                nc.vector.tensor_copy(
-                    out=self_grouped[:]
-                    .bitcast(F32)[:, g0 : g0 + BANK_GROUPS]
-                    .rearrange("p g r u -> p (g r) u"),
-                    in_=banks[(t, SELF, half)][:].rearrange("p u g r -> p (g r) u"),
-                )
-                nc.scalar.activation(
-                    out=neigh_grouped[:, g0 : g0 + BANK_GROUPS].rearrange(
-                        "p g r (u e) -> p (g r) u e", e=2
-                    ),
-                    in_=banks[(t, NEIGH, half)][:]
-                    .bitcast(BF16)
-                    .rearrange("p u g (r e) -> p (g r) u e", e=2),
-                    func=ACT.Copy,
-                    scale=0.5,
-                )
+        def leave_psum(s):
+            groups = steps[s][3]
+            self_grouped = grouped_pool.tile([P, groups, P, PACK], BF16, align_bytes=64)
+            neigh_grouped = grouped_pool.tile([P, groups, P, PACK], BF16, align_bytes=64)
+            grouped[(s, SELF)] = self_grouped
+            grouped[(s, NEIGH)] = neigh_grouped
+            for op, leave in ((SELF, nc.scalar.copy), (NEIGH, nc.scalar.copy)):
+                for b0 in range(0, groups, BANK_GROUPS):
+                    b1 = min(b0 + BANK_GROUPS, groups)
+                    leave(
+                        out=grouped[(s, op)][:].bitcast(F32)[:, b0:b1].rearrange("p g r u -> p (g r) u"),
+                        in_=banks[(s, op, b0)][:].rearrange("p u g r -> p (g r) u"),
+                    )
 
-        def quantise(t, op):
-            code = code_pool.tile([P, CHUNK_GROUPS, P], U32, align_bytes=64, tag="code%d" % op)
-            code_scale = code_pool.tile([P, CHUNK_GROUPS, P], U8, align_bytes=64, tag="scale%d" % op)
+        def quantise(s, op):
+            groups = steps[s][3]
+            code = code_pool.tile([P, groups, P], U32, align_bytes=64, tag="code%d" % op)
+            code_scale = code_pool.tile([P, groups, P], U8, align_bytes=64, tag="scale%d" % op)
             nc.vector.quantize_mx(
                 out=code[:].rearrange("p g r -> p (g r)").bitcast(FP8X4),
                 scales=code_scale[:].rearrange("p g r -> p (g r)"),
-                in_=grouped[(t, op)][:].rearrange("p g r t -> p (g r t)"),
+                in_=grouped[(s, op)][:].rearrange("p g r t -> p (g r t)"),
             )
-            codes[(t, op)] = code
-            code_scales[(t, op)] = code_scale
+            codes[(s, op)] = code
+            code_scales[(s, op)] = code_scale
 
-        def passes(t):
-            c, i = divmod(t, ITEM_TILES)
+        def passes(s):
+            c, i, g0, groups = steps[s]
             for op in OPERANDS:
-                for gi in range(CHUNK_GROUPS):
-                    g = c * CHUNK_GROUPS + gi
+                for gi in range(groups):
+                    g = g0 + gi
                     nc.tensor.matmul_mx(
-                        out=acc[i][:],
-                        lhsT=codes[(t, op)][:, gi, :].bitcast(FP8X4),
-                        lhsT_scale=code_scales[(t, op)][:, gi, :],
-                        rhs=w_tiles[(c, op)][:, gi, :].bitcast(FP4X4),
+                        out=acc[(i, op)][:],
+                        lhsT=codes[(s, op)][:, gi, :].bitcast(FP8X4),
+                        lhsT_scale=code_scales[(s, op)][:, gi, :],
+                        rhs=w_tiles[(c, op)][:, g - chunks[c][0], :].bitcast(FP4X4),
                         rhs_scale=w_scales[g // QUARTER_GROUPS][:, op, g % QUARTER_GROUPS, :],
-                        start=(g == 0 and op == OPERANDS[0]),
-                        stop=(g == GROUPS - 1 and op == OPERANDS[-1]),
+                        start=(s == first_step[i] and gi == 0),
+                        stop=(s == last_step[i] and gi == groups - 1),
                     )
+            if last_w_use[c] == s:
+                live["w"] = live["w"] - len(OPERANDS)
 
         w_scales = []
         for quarter in range(QUARTERS):
@@ -186,13 +226,10 @@ def tile_dogtaitujuanji_pb_k_kernel(
             nc.vector.memset(plane[:].bitcast(I32), 0)
             w_scales.append(plane)
 
-        for quarter in range(QUARTERS):
-            for n in range(QUARTER_DMAS):
-                load_scale_rows(quarter, n)
-
-        for c in range(AHEAD):
-            load_h(c)
-            load_weights(c)
+        pending.extend([("w", 0, SELF), ("w", 0, NEIGH), ("scales", 0, 0), ("h", 0, 0), ("h", 0, 1)])
+        for c in range(1, len(chunks)):
+            pending.extend([("h", c, 0), ("h", c, 1), ("w", c, SELF), ("w", c, NEIGH)])
+        issue_loads()
 
         ident = const.tile([P, P], F32)
         make_identity(nc, ident[:])
@@ -211,92 +248,134 @@ def tile_dogtaitujuanji_pb_k_kernel(
             out=gb_rows[COL_TILES : 2 * COL_TILES, :], in_=beta.rearrange("(j p) -> j p", p=P)
         )
 
-        acc = []
+        acc = {}
         for i in range(ITEM_TILES):
-            acc.append(acc_pool.tile([P, COLS], F32, name="acc%d" % i))
-
-        add_hops(0)
-        split_self(0)
-        for t in range(STEPS + 1):
-            if t % ITEM_TILES == 0 and t // ITEM_TILES + AHEAD < CHUNKS:
-                load_h(t // ITEM_TILES + AHEAD)
-                load_weights(t // ITEM_TILES + AHEAD)
-            if t < STEPS:
-                transposes(t)
-                leave_psum(t)
-                if t + 1 < STEPS:
-                    add_hops(t + 1)
-                    split_self(t + 1)
-                quantise(t, SELF)
-                quantise(t, NEIGH)
-            if t >= 1:
-                passes(t - 1)
+            for op in OPERANDS:
+                acc[(i, op)] = acc_pool.tile([P, COLS], F32, name="acc%d%d" % (i, op))
 
         gb_rows_f32 = const.tile([P, P], F32)
         nc.vector.tensor_copy(out=gb_rows_f32[:], in_=gb_rows[:])
-
-        y_rows = []
-        for i in range(ITEM_TILES):
-            y_rows.append(const.tile([P, COLS], F32, name="y_rows%d" % i))
-        for i in range(ITEM_TILES):
-            nc.scalar.copy(out=y_rows[i][:], in_=acc[i][:])
-
         gb_bank = bank_pool.tile([P, P], F32, tag="bank")
         nc.tensor.transpose(gb_bank[:], gb_rows_f32[:], ident[:])
         gamma_beta = const.tile([P, 2 * COL_TILES], F32)
         nc.vector.tensor_copy(out=gamma_beta[:], in_=gb_bank[:, 0 : 2 * COL_TILES])
 
+        split_self(0)
+        add_hops(0)
+        for s in range(n_steps + 1):
+            issue_loads()
+            if s < n_steps:
+                transposes(s)
+                leave_psum(s)
+                if s + 1 < n_steps:
+                    split_self(s + 1)
+                    add_hops(s + 1)
+                    issue_loads()
+                quantise(s, SELF)
+                quantise(s, NEIGH)
+            if s >= 1:
+                passes(s - 1)
+
+        self_rows = []
+        y_rows = []
+        for i in range(ITEM_TILES):
+            self_rows.append(const.tile([P, COLS], F32, name="self_rows%d" % i))
+            y_rows.append(const.tile([P, COLS], F32, name="y_rows%d" % i))
         y_cols = []
         for j in range(COL_TILES):
             y_cols.append(bank_pool.tile([P, ITEMS], F32, tag="bank", name="y_cols%d" % j))
         stats = const.tile([P, COL_TILES, ITEM_TILES, 6], F32)
+        mean_var = const.tile([P, COL_TILES, 2], F32)
+        var_eps = const.tile([P, COL_TILES], F32)
+        rstd = const.tile([P, COL_TILES], F32)
+        mean_gamma = const.tile([P, COL_TILES], F32)
+        mean_gain = const.tile([P, COL_TILES], F32)
+        gain = const.tile([P, COL_TILES], F32)
+        shift = const.tile([P, COL_TILES], F32)
+        out_cols = const.tile([P, COL_TILES, ITEMS], F32)
+
+        def pair(half):
+            return slice(half * PAIR, (half + 1) * PAIR)
+
         for i in range(ITEM_TILES):
+            nc.scalar.copy(out=self_rows[i][:], in_=acc[(i, SELF)][:])
+            for half in range(HALVES):
+                cols = slice(half * PAIR * P, (half + 1) * PAIR * P)
+                nc.vector.scalar_tensor_tensor(
+                    out=y_rows[i][:, cols],
+                    in0=acc[(i, NEIGH)][:, cols],
+                    scalar=0.5,
+                    in1=self_rows[i][:, cols],
+                    op0=ALU.mult,
+                    op1=ALU.add,
+                )
             for j in range(COL_TILES):
                 nc.tensor.transpose(
                     y_cols[j][:, i * P : (i + 1) * P], y_rows[i][:, j * P : (j + 1) * P], ident[:]
                 )
-            for j in range(COL_TILES):
-                nc.vector.bn_stats(out=stats[:, j, i, :], in_=y_cols[j][:, i * P : (i + 1) * P])
-        mean_var = const.tile([P, COL_TILES, 2], F32)
-        for j in range(COL_TILES):
-            nc.vector.bn_aggr(
-                out=mean_var[:, j, :], in_=stats[:, j, :, :].rearrange("p i s -> p (i s)")
-            )
+            if i < ITEM_TILES - 1:
+                for j in range(COL_TILES):
+                    nc.vector.bn_stats(out=stats[:, j, i, :], in_=y_cols[j][:, i * P : (i + 1) * P])
 
-        var_eps = const.tile([P, COL_TILES], F32)
-        nc.vector.tensor_scalar_add(out=var_eps[:], in0=mean_var[:, :, 1], scalar1=BN_EPS)
-        rstd = const.tile([P, COL_TILES], F32)
-        nc.gpsimd.tensor_tensor(out=rstd[:], in0=var_eps[:], in1=minus_half[:], op=ALU.pow)
-        mean_gamma = const.tile([P, COL_TILES], F32)
-        nc.vector.tensor_mul(out=mean_gamma[:], in0=mean_var[:, :, 0], in1=gamma_beta[:, 0:COL_TILES])
-        mean_gain = const.tile([P, COL_TILES], F32)
-        nc.vector.tensor_mul(out=mean_gain[:], in0=mean_gamma[:], in1=rstd[:])
-        gain = const.tile([P, COL_TILES], F32)
-        nc.vector.tensor_mul(out=gain[:], in0=gamma_beta[:, 0:COL_TILES], in1=rstd[:])
-        shift = const.tile([P, COL_TILES], F32)
-        nc.vector.tensor_sub(out=shift[:], in0=gamma_beta[:, COL_TILES : 2 * COL_TILES], in1=mean_gain[:])
-
-        out_cols = const.tile([P, COL_TILES, ITEMS], F32)
-        out_banks = []
-        for i in range(ITEM_TILES):
-            out_banks.append(bank_pool.tile([P, COLS], F32, tag="bank", name="out_bank%d" % i))
-        for j in range(COL_TILES):
-            nc.scalar.activation(
-                out=out_cols[:, j, :],
-                in_=y_cols[j][:],
-                func=ACT.Sigmoid,
-                bias=shift[:, j : j + 1],
-                scale=gain[:, j : j + 1],
-            )
-            for i in range(ITEM_TILES):
-                nc.tensor.transpose(
-                    out_banks[i][:, j * P : (j + 1) * P], out_cols[:, j, i * P : (i + 1) * P], ident[:]
+        last = ITEM_TILES - 1
+        for half in range(HALVES):
+            for j in range(half * PAIR, (half + 1) * PAIR):
+                nc.vector.bn_stats(out=stats[:, j, last, :], in_=y_cols[j][:, last * P : (last + 1) * P])
+            for j in range(half * PAIR, (half + 1) * PAIR):
+                nc.vector.bn_aggr(
+                    out=mean_var[:, j, :], in_=stats[:, j, :, :].rearrange("p i s -> p (i s)")
                 )
+            nc.vector.tensor_scalar_add(
+                out=var_eps[:, pair(half)], in0=mean_var[:, pair(half), 1], scalar1=BN_EPS
+            )
+            nc.gpsimd.tensor_tensor(
+                out=rstd[:, pair(half)], in0=var_eps[:, pair(half)], in1=minus_half[:, pair(half)], op=ALU.pow
+            )
+            nc.vector.tensor_mul(
+                out=mean_gamma[:, pair(half)], in0=mean_var[:, pair(half), 0], in1=gamma_beta[:, pair(half)]
+            )
 
-        out_rows = []
+        out_banks = {}
+        out_rows = {}
         for i in range(ITEM_TILES):
-            out_rows.append(const.tile([P, COLS], F32, name="out_rows%d" % i))
-        nc.vector.tensor_copy(out=out_rows[0][:], in_=out_banks[0][:])
-        nc.scalar.copy(out=out_rows[1][:], in_=out_banks[1][:])
-        for i in range(ITEM_TILES):
-            nc.sync.dma_start(out=out[i * P : (i + 1) * P, :], in_=out_rows[i][:])
+            for half in range(HALVES):
+                out_banks[(i, half)] = acc_pool.tile([P, PAIR * P], F32, name="acc%d%d" % (i, half))
+                out_rows[(i, half)] = const.tile([P, PAIR * P], F32, name="out_rows%d%d" % (i, half))
+        for half in range(HALVES):
+            nc.vector.tensor_mul(
+                out=mean_gain[:, pair(half)], in0=mean_gamma[:, pair(half)], in1=rstd[:, pair(half)]
+            )
+            nc.vector.tensor_mul(
+                out=gain[:, pair(half)], in0=gamma_beta[:, pair(half)], in1=rstd[:, pair(half)]
+            )
+            nc.vector.tensor_sub(
+                out=shift[:, pair(half)],
+                in0=gamma_beta[:, COL_TILES + half * PAIR : COL_TILES + (half + 1) * PAIR],
+                in1=mean_gain[:, pair(half)],
+            )
+            for j in range(half * PAIR, (half + 1) * PAIR):
+                nc.scalar.activation(
+                    out=out_cols[:, j, :],
+                    in_=y_cols[j][:],
+                    func=ACT.Sigmoid,
+                    bias=shift[:, j : j + 1],
+                    scale=gain[:, j : j + 1],
+                )
+                for i in range(ITEM_TILES):
+                    nc.tensor.transpose(
+                        out_banks[(i, half)][:, (j - half * PAIR) * P : (j - half * PAIR + 1) * P],
+                        out_cols[:, j, i * P : (i + 1) * P],
+                        ident[:],
+                    )
+        for half in range(HALVES):
+            for i in range(ITEM_TILES):
+                if half == HALVES - 1 and i == ITEM_TILES - 1:
+                    nc.scalar.copy(out=out_rows[(i, half)][:], in_=out_banks[(i, half)][:])
+                    queue = nc.scalar
+                else:
+                    nc.vector.tensor_copy(out=out_rows[(i, half)][:], in_=out_banks[(i, half)][:])
+                    queue = nc.sync
+                queue.dma_start(
+                    out=out[i * P : (i + 1) * P, half * PAIR * P : (half + 1) * PAIR * P],
+                    in_=out_rows[(i, half)][:],
+                )

from contextlib import ExitStack

import concourse.mybir as mybir
from concourse.masks import make_identity

F32 = mybir.dt.float32
BF16 = mybir.dt.bfloat16
I32 = mybir.dt.int32
U32 = mybir.dt.uint32
U8 = mybir.dt.uint8
FP8X4 = mybir.dt.float8_e4m3fn_x4
FP4X4 = mybir.dt.float4_e2m1fn_x4
ACT = mybir.ActivationFunctionType
ALU = mybir.AluOpType

P = 128
PACK = 4
GROUP_K = P * PACK
ITEMS = 256
ITEM_TILES = ITEMS // P
HOPS = 3
FEATURES = 16384
COLS = 512
COL_TILES = COLS // P
HALVES = 2
PAIR = COL_TILES // HALVES
BN_EPS = 1e-5

GROUPS = FEATURES // GROUP_K
BANK_GROUPS = 2
QUARTER_GROUPS = 8
QUARTERS = GROUPS // QUARTER_GROUPS
QUARTER_DMAS = 8

SELF = 0
NEIGH = 1
OPERANDS = (SELF, NEIGH)

FLOPS = 2 * 2 * ITEMS * FEATURES * COLS

LOAD_PLAN = (4, 4, 4, 4, 4, 4, 4, 4)
STEP_GROUPS = 4
H_BUFS = 6
W_BUFS = 8


def tile_dogtaitujuanji_pb_k_kernel(
    tc, h_sage, w1b_words, w1b_scales, w2b_words, w2b_scales, gamma, beta, out
):
    nc = tc.nc
    words_dram = (w2b_words, w1b_words)
    scales_dram = (w2b_scales, w1b_scales)

    chunks = []
    for groups in LOAD_PLAN:
        chunks.append((sum(n for g, n in chunks), groups))
    steps = []
    for c, (c0, groups) in enumerate(chunks):
        for i in range(ITEM_TILES):
            for g0 in range(c0, c0 + groups, STEP_GROUPS):
                steps.append((c, i, g0, min(STEP_GROUPS, c0 + groups - g0)))
    n_steps = len(steps)
    first_step = [min(s for s in range(n_steps) if steps[s][1] == i) for i in range(ITEM_TILES)]
    last_step = [max(s for s in range(n_steps) if steps[s][1] == i) for i in range(ITEM_TILES)]
    last_h_use = {}
    last_w_use = {}
    for s, (c, i, g0, groups) in enumerate(steps):
        last_h_use[(c, i)] = s
        last_w_use[c] = s

    with ExitStack() as stack:
        const = stack.enter_context(tc.tile_pool(name="const", bufs=1))
        h_pool = stack.enter_context(tc.tile_pool(name="h", bufs=H_BUFS))
        w_pool = stack.enter_context(tc.tile_pool(name="w", bufs=W_BUFS))
        split_pool = stack.enter_context(tc.tile_pool(name="split", bufs=3))
        grouped_pool = stack.enter_context(tc.tile_pool(name="grouped", bufs=3))
        code_pool = stack.enter_context(tc.tile_pool(name="codes", bufs=3))
        acc_pool = stack.enter_context(tc.psum_pool(name="acc", bufs=1))
        bank_pool = stack.enter_context(tc.psum_pool(name="banks", bufs=4))
        stack.enter_context(tc.manual_schedule())

        h_tiles = {}
        w_tiles = {}
        split_words = {}
        banks = {}
        grouped = {}
        codes = {}
        code_scales = {}
        live = {"h": 0, "w": 0, "issued": 0}
        pending = []

        def load_h(c, i):
            c0, groups = chunks[c]
            h_tile = h_pool.tile([P, HOPS, groups * GROUP_K], BF16)
            queue = nc.sync if i == 0 else nc.sync
            queue.dma_start(
                out=h_tile[:],
                in_=h_sage[i * P : (i + 1) * P, :, c0 * GROUP_K : (c0 + groups) * GROUP_K],
            )
            h_tiles[(c, i)] = h_tile

        def load_scale_rows(quarter, n):
            op, r = divmod(n, 4)
            g0 = quarter * QUARTER_GROUPS
            nc.sync.dma_start(
                out=w_scales[quarter][r:P:32, op, :, :].bitcast(I32),
                in_=scales_dram[op][g0 : g0 + QUARTER_GROUPS, r:16:4, :]
                .rearrange("g q n -> q g n")
                .bitcast(I32),
            )

        def load_weights(c, op):
            c0, groups = chunks[c]
            w_tile = w_pool.tile([P, groups, 2 * COLS], U8, align_bytes=64)
            nc.sync.dma_start(
                out=w_tile[:].bitcast(I32),
                in_=words_dram[op][c0 : c0 + groups].rearrange("g p b -> p g b").bitcast(I32),
            )
            w_tiles[(c, op)] = w_tile

        def issue_loads():
            while live["issued"] < len(pending):
                kind, c, x = pending[live["issued"]]
                if kind == "h":
                    if live["h"] == H_BUFS:
                        return
                    load_h(c, x)
                    live["h"] = live["h"] + 1
                elif kind == "w":
                    if live["w"] == W_BUFS:
                        return
                    load_weights(c, x)
                    live["w"] = live["w"] + 1
                else:
                    for quarter in range(QUARTERS):
                        for n in range(QUARTER_DMAS):
                            load_scale_rows(quarter, n)
                live["issued"] = live["issued"] + 1

        def add_hops(s):
            c, i, g0, groups = steps[s]
            k0 = (g0 - chunks[c][0]) * GROUP_K
            k1 = k0 + groups * GROUP_K
            hop_sum = split_pool.tile([P, 2, groups * P, 2], BF16)
            nc.vector.tensor_add(
                out=hop_sum[:],
                in0=h_tiles[(c, i)][:, 1, k0:k1].rearrange("p (w u e) -> p u w e", u=2, e=2),
                in1=h_tiles[(c, i)][:, 2, k0:k1].rearrange("p (w u e) -> p u w e", u=2, e=2),
            )
            split_words[(s, NEIGH)] = hop_sum[:].rearrange("p u w e -> p u (w e)").bitcast(F32)
            if last_h_use[(c, i)] == s:
                live["h"] = live["h"] - 1

        def split_self(s):
            c, i, g0, groups = steps[s]
            k0 = (g0 - chunks[c][0]) * GROUP_K
            k1 = k0 + groups * GROUP_K
            self_split = split_pool.tile([P, 2, groups * P], F32)
            nc.vector.tensor_copy(
                out=self_split[:],
                in_=h_tiles[(c, i)][:, 0, k0:k1].bitcast(F32).rearrange("p (w u) -> p u w", u=2),
            )
            split_words[(s, SELF)] = self_split[:]

        def transposes(s):
            groups = steps[s][3]
            for op in OPERANDS:
                words = split_words[(s, op)]
                for b0 in range(0, groups, BANK_GROUPS):
                    in_bank = min(BANK_GROUPS, groups - b0)
                    bank = bank_pool.tile([P, 2, in_bank, P], F32)
                    for gi in range(in_bank):
                        w0 = (b0 + gi) * P
                        for u in range(2):
                            nc.tensor.transpose(bank[:, u, gi, :], words[:, u, w0 : w0 + P], ident[:])
                    banks[(s, op, b0)] = bank

        def leave_psum(s):
            groups = steps[s][3]
            self_grouped = grouped_pool.tile([P, groups, P, PACK], BF16, align_bytes=64)
            neigh_grouped = grouped_pool.tile([P, groups, P, PACK], BF16, align_bytes=64)
            grouped[(s, SELF)] = self_grouped
            grouped[(s, NEIGH)] = neigh_grouped
            for op, leave in ((SELF, nc.scalar.copy), (NEIGH, nc.scalar.copy)):
                for b0 in range(0, groups, BANK_GROUPS):
                    b1 = min(b0 + BANK_GROUPS, groups)
                    leave(
                        out=grouped[(s, op)][:].bitcast(F32)[:, b0:b1].rearrange("p g r u -> p (g r) u"),
                        in_=banks[(s, op, b0)][:].rearrange("p u g r -> p (g r) u"),
                    )

        def quantise(s, op):
            groups = steps[s][3]
            code = code_pool.tile([P, groups, P], U32, align_bytes=64, tag="code%d" % op)
            code_scale = code_pool.tile([P, groups, P], U8, align_bytes=64, tag="scale%d" % op)
            nc.vector.quantize_mx(
                out=code[:].rearrange("p g r -> p (g r)").bitcast(FP8X4),
                scales=code_scale[:].rearrange("p g r -> p (g r)"),
                in_=grouped[(s, op)][:].rearrange("p g r t -> p (g r t)"),
            )
            codes[(s, op)] = code
            code_scales[(s, op)] = code_scale

        def passes(s):
            c, i, g0, groups = steps[s]
            for op in OPERANDS:
                for gi in range(groups):
                    g = g0 + gi
                    nc.tensor.matmul_mx(
                        out=acc[(i, op)][:],
                        lhsT=codes[(s, op)][:, gi, :].bitcast(FP8X4),
                        lhsT_scale=code_scales[(s, op)][:, gi, :],
                        rhs=w_tiles[(c, op)][:, g - chunks[c][0], :].bitcast(FP4X4),
                        rhs_scale=w_scales[g // QUARTER_GROUPS][:, op, g % QUARTER_GROUPS, :],
                        start=(s == first_step[i] and gi == 0),
                        stop=(s == last_step[i] and gi == groups - 1),
                    )
            if last_w_use[c] == s:
                live["w"] = live["w"] - len(OPERANDS)

        w_scales = []
        for quarter in range(QUARTERS):
            plane = const.tile(
                [P, len(OPERANDS), QUARTER_GROUPS, COLS], U8, align_bytes=64, name="plane%d" % quarter
            )
            nc.vector.memset(plane[:].bitcast(I32), 0)
            w_scales.append(plane)

        pending.extend([("w", 0, SELF), ("w", 0, NEIGH), ("scales", 0, 0), ("h", 0, 0), ("h", 0, 1)])
        for c in range(1, len(chunks)):
            pending.extend([("h", c, 0), ("h", c, 1), ("w", c, SELF), ("w", c, NEIGH)])
        issue_loads()

        ident = const.tile([P, P], F32)
        make_identity(nc, ident[:])

        warm = const.tile([P, 1], F32)
        nc.vector.memset(warm[:], 0.0)
        nc.scalar.activation(out=warm[:], in_=warm[:], func=ACT.Sigmoid)

        minus_half = const.tile([P, COL_TILES], F32)
        nc.vector.memset(minus_half[:], -0.5)

        gb_rows = const.tile([P, P], BF16)
        nc.vector.memset(gb_rows[:], 0.0)
        nc.scalar.dma_start(out=gb_rows[0:COL_TILES, :], in_=gamma.rearrange("(j p) -> j p", p=P))
        nc.scalar.dma_start(
            out=gb_rows[COL_TILES : 2 * COL_TILES, :], in_=beta.rearrange("(j p) -> j p", p=P)
        )

        acc = {}
        for i in range(ITEM_TILES):
            for op in OPERANDS:
                acc[(i, op)] = acc_pool.tile([P, COLS], F32, name="acc%d%d" % (i, op))

        gb_rows_f32 = const.tile([P, P], F32)
        nc.vector.tensor_copy(out=gb_rows_f32[:], in_=gb_rows[:])
        gb_bank = bank_pool.tile([P, P], F32, tag="bank")
        nc.tensor.transpose(gb_bank[:], gb_rows_f32[:], ident[:])
        gamma_beta = const.tile([P, 2 * COL_TILES], F32)
        nc.vector.tensor_copy(out=gamma_beta[:], in_=gb_bank[:, 0 : 2 * COL_TILES])

        split_self(0)
        add_hops(0)
        for s in range(n_steps + 1):
            issue_loads()
            if s < n_steps:
                transposes(s)
                leave_psum(s)
                if s + 1 < n_steps:
                    split_self(s + 1)
                    add_hops(s + 1)
                    issue_loads()
                quantise(s, SELF)
                quantise(s, NEIGH)
            if s >= 1:
                passes(s - 1)

        self_rows = []
        y_rows = []
        for i in range(ITEM_TILES):
            self_rows.append(const.tile([P, COLS], F32, name="self_rows%d" % i))
            y_rows.append(const.tile([P, COLS], F32, name="y_rows%d" % i))
        y_cols = []
        for j in range(COL_TILES):
            y_cols.append(bank_pool.tile([P, ITEMS], F32, tag="bank", name="y_cols%d" % j))
        stats = const.tile([P, COL_TILES, ITEM_TILES, 6], F32)
        mean_var = const.tile([P, COL_TILES, 2], F32)
        var_eps = const.tile([P, COL_TILES], F32)
        rstd = const.tile([P, COL_TILES], F32)
        mean_gamma = const.tile([P, COL_TILES], F32)
        mean_gain = const.tile([P, COL_TILES], F32)
        gain = const.tile([P, COL_TILES], F32)
        shift = const.tile([P, COL_TILES], F32)
        out_cols = const.tile([P, COL_TILES, ITEMS], F32)

        def pair(half):
            return slice(half * PAIR, (half + 1) * PAIR)

        for i in range(ITEM_TILES):
            nc.scalar.copy(out=self_rows[i][:], in_=acc[(i, SELF)][:])
            for half in range(HALVES):
                cols = slice(half * PAIR * P, (half + 1) * PAIR * P)
                nc.vector.scalar_tensor_tensor(
                    out=y_rows[i][:, cols],
                    in0=acc[(i, NEIGH)][:, cols],
                    scalar=0.5,
                    in1=self_rows[i][:, cols],
                    op0=ALU.mult,
                    op1=ALU.add,
                )
            for j in range(COL_TILES):
                nc.tensor.transpose(
                    y_cols[j][:, i * P : (i + 1) * P], y_rows[i][:, j * P : (j + 1) * P], ident[:]
                )
            if i < ITEM_TILES - 1:
                for j in range(COL_TILES):
                    nc.vector.bn_stats(out=stats[:, j, i, :], in_=y_cols[j][:, i * P : (i + 1) * P])

        last = ITEM_TILES - 1
        for half in range(HALVES):
            for j in range(half * PAIR, (half + 1) * PAIR):
                nc.vector.bn_stats(out=stats[:, j, last, :], in_=y_cols[j][:, last * P : (last + 1) * P])
            for j in range(half * PAIR, (half + 1) * PAIR):
                nc.vector.bn_aggr(
                    out=mean_var[:, j, :], in_=stats[:, j, :, :].rearrange("p i s -> p (i s)")
                )
            nc.vector.tensor_scalar_add(
                out=var_eps[:, pair(half)], in0=mean_var[:, pair(half), 1], scalar1=BN_EPS
            )
            nc.gpsimd.tensor_tensor(
                out=rstd[:, pair(half)], in0=var_eps[:, pair(half)], in1=minus_half[:, pair(half)], op=ALU.pow
            )
            nc.vector.tensor_mul(
                out=mean_gamma[:, pair(half)], in0=mean_var[:, pair(half), 0], in1=gamma_beta[:, pair(half)]
            )

        out_banks = {}
        out_rows = {}
        for i in range(ITEM_TILES):
            for half in range(HALVES):
                out_banks[(i, half)] = acc_pool.tile([P, PAIR * P], F32, name="acc%d%d" % (i, half))
                out_rows[(i, half)] = const.tile([P, PAIR * P], F32, name="out_rows%d%d" % (i, half))
        for half in range(HALVES):
            nc.vector.tensor_mul(
                out=mean_gain[:, pair(half)], in0=mean_gamma[:, pair(half)], in1=rstd[:, pair(half)]
            )
            nc.vector.tensor_mul(
                out=gain[:, pair(half)], in0=gamma_beta[:, pair(half)], in1=rstd[:, pair(half)]
            )
            nc.vector.tensor_sub(
                out=shift[:, pair(half)],
                in0=gamma_beta[:, COL_TILES + half * PAIR : COL_TILES + (half + 1) * PAIR],
                in1=mean_gain[:, pair(half)],
            )
            for j in range(half * PAIR, (half + 1) * PAIR):
                nc.scalar.activation(
                    out=out_cols[:, j, :],
                    in_=y_cols[j][:],
                    func=ACT.Sigmoid,
                    bias=shift[:, j : j + 1],
                    scale=gain[:, j : j + 1],
                )
                for i in range(ITEM_TILES):
                    nc.tensor.transpose(
                        out_banks[(i, half)][:, (j - half * PAIR) * P : (j - half * PAIR + 1) * P],
                        out_cols[:, j, i * P : (i + 1) * P],
                        ident[:],
                    )
        for half in range(HALVES):
            for i in range(ITEM_TILES):
                if half == HALVES - 1 and i == ITEM_TILES - 1:
                    nc.scalar.copy(out=out_rows[(i, half)][:], in_=out_banks[(i, half)][:])
                    queue = nc.scalar
                else:
                    nc.vector.tensor_copy(out=out_rows[(i, half)][:], in_=out_banks[(i, half)][:])
                    queue = nc.sync
                queue.dma_start(
                    out=out[i * P : (i + 1) * P, half * PAIR * P : (half + 1) * PAIR * P],
                    in_=out_rows[(i, half)][:],
                )
